import numpy as np
import ml_dtypes


def mxq(x, axis, fmt="e4m3"):
    dtype, down = {"e4m3": (ml_dtypes.float8_e4m3fn, 7), "e5m2": (ml_dtypes.float8_e5m2, 14)}[fmt]
    v = np.moveaxis(np.asarray(x, np.float32).astype(ml_dtypes.bfloat16).astype(np.float64), axis, -1)
    blocks = v.reshape(v.shape[:-1] + (-1, 32))
    amax = np.abs(blocks).max(-1, keepdims=True)
    byte = np.maximum(np.where(amax > 0, np.frexp(amax)[1] - 1 + 127, 0) - down, 1)
    scale = np.exp2(byte - 127.0)
    codes = (blocks / scale).astype(np.float32).astype(dtype).astype(np.float64)
    return np.moveaxis((codes * scale).reshape(v.shape), -1, axis)


WIDE = False


def mx_kscale(k):
    if not WIDE:
        return np.ones(k)
    levels = np.array([10, -10, 5, -5, 0])
    a = np.random.permutation(np.resize(levels, k // 512 * 4)).reshape(k // 512, 4)
    idx = np.arange(k)
    return np.exp2(a[idx // 512, idx % 128 // 32])


BF16 = ml_dtypes.bfloat16


def bf(x):
    return np.asarray(x, np.float32).astype(BF16)


def f64(x):
    return np.asarray(x).astype(np.float64)


E2M1 = np.array([0.0, 0.5, 1.0, 1.5, 2.0, 3.0, 4.0, 6.0, -0.0, -0.5, -1.0, -1.5, -2.0, -3.0, -4.0, -6.0])


def pack_weight(w, fmt):
    k, n = w.shape
    w = f64(bf(w)).reshape(k // 32, 32, n)
    amax = np.abs(w).max(1)
    if fmt == "e4m3":
        byte = np.frexp(amax)[1] - 1 + 127 - 7
    else:
        mant, ex = np.frexp(amax / 6.0)
        byte = np.where(mant > 0.5, ex, ex - 1) + 127
    byte = np.clip(np.where(amax > 0, byte, 1), 1, 254)
    scaled = (w * np.exp2(127.0 - byte)[:, None, :]).reshape(k, n).astype(np.float32)
    by_word = np.ascontiguousarray(scaled.reshape(k // 512, 128, 4, n).transpose(0, 1, 3, 2))
    if fmt == "e4m3":
        words = by_word.astype(ml_dtypes.float8_e4m3fn).view(np.uint8)
    else:
        c = by_word.astype(ml_dtypes.float4_e2m1fn).view(np.uint8) & 0xF
        words = c[..., 0::2] | (c[..., 1::2] << 4)
    return np.ascontiguousarray(words), np.ascontiguousarray(byte.astype(np.uint8).reshape(k // 512, 16, n))


def unpack_weight(words, scales, fmt):
    g, p, n, _ = words.shape
    if fmt == "e4m3":
        vals = np.ascontiguousarray(words).view(ml_dtypes.float8_e4m3fn).astype(np.float64)
    else:
        nib = np.empty((g, p, n, 4), np.uint8)
        nib[..., 0::2] = words & 0xF
        nib[..., 1::2] = words >> 4
        vals = E2M1[nib]
    vals = vals * np.repeat(np.exp2(scales.astype(np.float64) - 127.0), 8, axis=1)[..., None]
    return vals.transpose(0, 1, 3, 2).reshape(g * 512, n)

def pack4(w):
    words, scales = pack_weight(w, "e2m1")
    return words.reshape(words.shape[0], 128, -1), scales


def unpack4(words, scales):
    return unpack_weight(words.reshape(words.shape[0], 128, -1, 2), scales, "e2m1")


B, IN, L = 4096, 1024, 256


def sigmoid(v):
    return 1.0 / (1.0 + np.exp(-v))


def setup_inputs():
    s = mx_kscale(IN)
    inp = bf(np.random.standard_normal((B, IN)) * s)
    h0 = bf(np.random.standard_normal((B, L)))
    gh0 = bf(np.random.standard_normal((B, 3 * L)) * 0.75)
    w = np.random.standard_normal((3 * L, IN)) * 0.7 / np.sqrt(IN) / s
    words, scales = pack4(w.T)
    b_ih0 = bf(np.random.standard_normal(3 * L) * 0.3)
    return {"input": inp,
            "h0": h0,
            "gh0": gh0,
            "W_ih0_words": words,
            "W_ih0_scales": scales,
            "b_ih0": b_ih0}


def reference(input, h0, gh0, W_ih0_words, W_ih0_scales, b_ih0):
    h, gh = f64(h0), f64(gh0)
    gi = (mxq(f64(input), 1, "e4m3") @ unpack4(W_ih0_words, W_ih0_scales)) + f64(b_ih0)
    i_r, i_z, i_n = gi[:, :L], gi[:, L:2 * L], gi[:, 2 * L:]
    h_r, h_z, h_n = gh[:, :L], gh[:, L:2 * L], gh[:, 2 * L:]
    r = sigmoid(i_r + h_r)
    z = sigmoid(i_z + h_z)
    n = np.tanh(i_n + r * h_n)
    return (1.0 - z) * n + z * h

@@ -1,0 +1,170 @@
+from contextlib import ExitStack
+
+import concourse.mybir as mybir
+from concourse.masks import make_identity
+
+F32 = mybir.dt.float32
+BF16 = mybir.dt.bfloat16
+I32 = mybir.dt.int32
+U32 = mybir.dt.uint32
+U8 = mybir.dt.uint8
+FP8X4 = mybir.dt.float8_e4m3fn_x4
+FP4X4 = mybir.dt.float4_e2m1fn_x4
+ACT = mybir.ActivationFunctionType
+ALU = mybir.AluOpType
+
+P = 128
+PACK = 4
+K_PASS = P * PACK
+
+ROWS, K, HIDDEN = 4096, 1024, 256
+GATES = 3 * HIDDEN
+PASSES = K // K_PASS
+GATE_TILES = GATES // P
+RZ_TILES = 2 * HIDDEN // P
+ROW_TILES = ROWS // P
+ROUND_TILES = 4
+ROUND_ROWS = ROUND_TILES * P
+ROUNDS = ROW_TILES // ROUND_TILES
+PAIR = 2
+WORDS = K // 2
+
+FLOPS = 2 * ROWS * K * GATES
+
+
+def tile_grucellstack_pa_t_kernel(tc, x, h0, gh0, w_words, w_scales, b_ih0, out):
+    nc = tc.nc
+
+    x_rows = x.rearrange("(p t) k -> p t k", t=ROW_TILES)
+    gh_rows = gh0.rearrange("(p t) c -> p t c", t=ROW_TILES)
+    h_rows = h0.rearrange("(p t) c -> p t c", t=ROW_TILES)
+    out_rows = out.rearrange("(p t) c -> p t c", t=ROW_TILES)
+
+    with ExitStack() as ctx:
+        const = ctx.enter_context(tc.tile_pool(name="const", bufs=1))
+        loads = ctx.enter_context(tc.tile_pool(name="loads", bufs=4))
+        quant = ctx.enter_context(tc.tile_pool(name="quant", bufs=2))
+        work = ctx.enter_context(tc.tile_pool(name="work", bufs=3))
+        psum_xt = ctx.enter_context(tc.psum_pool(name="psum_xt", bufs=2))
+        psum_git = ctx.enter_context(tc.psum_pool(name="psum_git", bufs=2))
+        psum_rz = ctx.enter_context(tc.psum_pool(name="psum_rz", bufs=2))
+        psum_n = ctx.enter_context(tc.psum_pool(name="psum_n", bufs=2))
+
+        def load_round(rnd):
+            tiles = slice(rnd * ROUND_TILES, (rnd + 1) * ROUND_TILES)
+            x_sb = loads.tile([P, ROUND_TILES, K], BF16)
+            nc.sync.dma_start(out=x_sb[:], in_=x_rows[:, tiles, :])
+            gh_sb = loads.tile([P, ROUND_TILES, GATES], BF16)
+            nc.sync.dma_start(out=gh_sb[:], in_=gh_rows[:, tiles, :])
+            h_sb = loads.tile([P, ROUND_TILES, HIDDEN], BF16)
+            nc.sync.dma_start(out=h_sb[:], in_=h_rows[:, tiles, :])
+            return x_sb, gh_sb, h_sb
+
+        first_loads = load_round(0)
+
+        ident = const.tile([P, P], F32)
+        make_identity(nc, ident[:])
+
+        w_codes = const.tile([P, PASSES, 2 * GATES], U8, align_bytes=64)
+        nc.sync.dma_start(
+            out=w_codes[:].bitcast(I32), in_=w_words.rearrange("g p b -> p g b").bitcast(I32)
+        )
+        w_planes = const.tile([P, PASSES, GATES], U8, align_bytes=64)
+        nc.vector.memset(w_planes[:].bitcast(I32), 0)
+        for quad in range(4):
+            nc.sync.dma_start(
+                out=w_planes[32 * quad : 32 * quad + 4].bitcast(I32),
+                in_=w_scales[:, 4 * quad : 4 * quad + 4, :].rearrange("g r n -> r g n").bitcast(I32),
+            )
+
+        bias_rows = const.tile([P, P], BF16)
+        nc.vector.memset(bias_rows[:], 0.0)
+        nc.sync.dma_start(out=bias_rows[0:GATE_TILES, :], in_=b_ih0.rearrange("(j c) -> j c", c=P))
+        bias_rows_f32 = const.tile([P, P], F32)
+        nc.vector.tensor_copy(out=bias_rows_f32[:], in_=bias_rows[:])
+        bias_ps = psum_n.tile([P, PAIR, HIDDEN], F32, tag="gi_n")
+        nc.tensor.transpose(bias_ps[:, 0, 0:P], bias_rows_f32[:], ident[:])
+        bias_col = const.tile([P, GATE_TILES], F32)
+        nc.vector.tensor_copy(out=bias_col[:], in_=bias_ps[:, 0, 0:GATE_TILES])
+
+        def quantise_round(x_sb):
+            grouped = quant.tile([P, PASSES, ROUND_ROWS, PACK], BF16, align_bytes=64)
+            grouped_words = grouped[:].bitcast(F32)
+            for i in range(ROUND_TILES):
+                x_words = x_sb[:, i, :].bitcast(F32)
+                xt = psum_xt.tile([P, PASSES, 2, P], F32)
+                for g in range(PASSES):
+                    for u in range(2):
+                        first = g * (WORDS // PASSES) + u
+                        last = (g + 1) * (WORDS // PASSES)
+                        nc.tensor.transpose(xt[:, g, u, :], x_words[:, first:last:2], ident[:])
+                nc.scalar.copy(
+                    out=grouped_words[:, :, i * P : (i + 1) * P, :],
+                    in_=xt[:].rearrange("p g u r -> p g r u"),
+                )
+            x_codes = quant.tile([P, PASSES, ROUND_ROWS], U32, align_bytes=64)
+            x_planes = quant.tile([P, PASSES, ROUND_ROWS], U8, align_bytes=64)
+            nc.vector.quantize_mx(
+                out=x_codes[:].rearrange("p g r -> p (g r)").bitcast(FP8X4),
+                scales=x_planes[:].rearrange("p g r -> p (g r)"),
+                in_=grouped[:].rearrange("p g r t -> p (g r t)"),
+            )
+            return x_codes, x_planes
+
+        def project_round(x_codes, x_planes):
+            gi_t = quant.tile([P, GATE_TILES, ROUND_ROWS], F32)
+            for j in range(GATE_TILES):
+                acc = psum_git.tile([P, ROUND_ROWS], F32)
+                for g in range(PASSES):
+                    nc.tensor.matmul_mx(
+                        out=acc[:],
+                        lhsT=w_codes[:, g, 2 * P * j : 2 * P * (j + 1)].bitcast(FP4X4),
+                        lhsT_scale=w_planes[:, g, P * j : P * (j + 1)],
+                        rhs=x_codes[:, g, :].bitcast(FP8X4),
+                        rhs_scale=x_planes[:, g, :],
+                        start=(g == 0),
+                        stop=(g == PASSES - 1),
+                    )
+                nc.scalar.activation(
+                    out=gi_t[:, j, :], in_=acc[:], func=ACT.Identity, bias=bias_col[:, j : j + 1]
+                )
+            return gi_t
+
+        def gates_round(rnd, gi_t, gh_sb, h_sb):
+            out_sb = work.tile([P, ROUND_TILES, HIDDEN], F32)
+            for first in range(0, ROUND_TILES, PAIR):
+                pair = slice(first, first + PAIR)
+                rz = work.tile([P, PAIR, 2 * HIDDEN], F32)
+                gi_n = psum_n.tile([P, PAIR, HIDDEN], F32, tag="gi_n")
+                for s in range(PAIR):
+                    rows = slice((first + s) * P, (first + s + 1) * P)
+                    gi_rz = psum_rz.tile([P, 2 * HIDDEN], F32)
+                    for j in range(RZ_TILES):
+                        nc.tensor.transpose(gi_rz[:, j * P : (j + 1) * P], gi_t[:, j, rows], ident[:])
+                    for j in range(RZ_TILES, GATE_TILES):
+                        cols = slice((j - RZ_TILES) * P, (j - RZ_TILES + 1) * P)
+                        nc.tensor.transpose(gi_n[:, s, cols], gi_t[:, j, rows], ident[:])
+                    nc.vector.tensor_tensor(
+                        out=rz[:, s, :], in0=gi_rz[:], in1=gh_sb[:, first + s, 0 : 2 * HIDDEN], op=ALU.add
+                    )
+                nc.scalar.activation(out=rz[:], in_=rz[:], func=ACT.Sigmoid)
+                r_gate = rz[:, :, 0:HIDDEN]
+                z_gate = rz[:, :, HIDDEN : 2 * HIDDEN]
+                n_gate = work.tile([P, PAIR, HIDDEN], F32)
+                nc.vector.tensor_tensor(
+                    out=n_gate[:], in0=r_gate, in1=gh_sb[:, pair, 2 * HIDDEN : GATES], op=ALU.mult
+                )
+                nc.vector.tensor_tensor(out=n_gate[:], in0=gi_n[:], in1=n_gate[:], op=ALU.add)
+                nc.scalar.activation(out=n_gate[:], in_=n_gate[:], func=ACT.Tanh)
+                diff = work.tile([P, PAIR, HIDDEN], F32)
+                nc.vector.tensor_tensor(out=diff[:], in0=h_sb[:, pair, :], in1=n_gate[:], op=ALU.subtract)
+                nc.vector.tensor_tensor(out=diff[:], in0=z_gate, in1=diff[:], op=ALU.mult)
+                nc.vector.tensor_tensor(out=out_sb[:, pair, :], in0=diff[:], in1=n_gate[:], op=ALU.add)
+            tiles = slice(rnd * ROUND_TILES, (rnd + 1) * ROUND_TILES)
+            nc.sync.dma_start(out=out_rows[:, tiles, :], in_=out_sb[:])
+
+        for rnd in range(ROUNDS):
+            x_sb, gh_sb, h_sb = first_loads if rnd == 0 else load_round(rnd)
+            x_codes, x_planes = quantise_round(x_sb)
+            gi_t = project_round(x_codes, x_planes)
+            gates_round(rnd, gi_t, gh_sb, h_sb)

@@ -20,14 +20,24 @@ K_PASS = P * PACK
 ROWS, K, HIDDEN = 4096, 1024, 256
 GATES = 3 * HIDDEN
 PASSES = K // K_PASS
+PASS_WORDS = K_PASS // 2
 GATE_TILES = GATES // P
 RZ_TILES = 2 * HIDDEN // P
 ROW_TILES = ROWS // P
-ROUND_TILES = 4
-ROUND_ROWS = ROUND_TILES * P
-ROUNDS = ROW_TILES // ROUND_TILES
 PAIR = 2
-WORDS = K // 2
+HALF_ROWS = PAIR * P
+ROUND_ROWS = 2 * HALF_ROWS
+ROUNDS = ROWS // ROUND_ROWS
+HALVES = 2 * ROUNDS
+
+X_LEAD = 2
+ADD_LAG = 2
+SIGMOID_LAG = 3
+CANDIDATE_LAG = 3
+TANH_LAG = 4
+BLEND_LAG = 5
+X_LOAD_LEAD = 4
+GH_LOAD_LEAD = 4
 
 FLOPS = 2 * ROWS * K * GATES
 
@@ -42,28 +52,40 @@ def tile_grucellstack_pa_t_kernel(tc, x, h0, gh0, w_words, w_scales, b_ih0, out)
 
     with ExitStack() as ctx:
         const = ctx.enter_context(tc.tile_pool(name="const", bufs=1))
-        loads = ctx.enter_context(tc.tile_pool(name="loads", bufs=4))
+        x_pool = ctx.enter_context(tc.tile_pool(name="x_pool", bufs=X_LOAD_LEAD + 2))
+        gh_pool = ctx.enter_context(tc.tile_pool(name="gh_pool", bufs=(GH_LOAD_LEAD + BLEND_LAG) // 2 + 1))
         quant = ctx.enter_context(tc.tile_pool(name="quant", bufs=2))
-        work = ctx.enter_context(tc.tile_pool(name="work", bufs=3))
+        git_pool = ctx.enter_context(tc.tile_pool(name="git_pool", bufs=3))
+        work = ctx.enter_context(tc.tile_pool(name="work", bufs=BLEND_LAG - ADD_LAG + 1))
         psum_xt = ctx.enter_context(tc.psum_pool(name="psum_xt", bufs=2))
-        psum_git = ctx.enter_context(tc.psum_pool(name="psum_git", bufs=2))
+        psum_git = ctx.enter_context(tc.psum_pool(name="psum_git", bufs=3))
         psum_rz = ctx.enter_context(tc.psum_pool(name="psum_rz", bufs=2))
-        psum_n = ctx.enter_context(tc.psum_pool(name="psum_n", bufs=2))
+        psum_n = ctx.enter_context(tc.psum_pool(name="psum_n", bufs=1))
+        ctx.enter_context(tc.manual_schedule())
 
-        def load_round(rnd):
-            tiles = slice(rnd * ROUND_TILES, (rnd + 1) * ROUND_TILES)
-            x_sb = loads.tile([P, ROUND_TILES, K], BF16)
-            nc.sync.dma_start(out=x_sb[:], in_=x_rows[:, tiles, :])
-            gh_sb = loads.tile([P, ROUND_TILES, GATES], BF16)
+        x_of, gh_of, h_of = {}, {}, {}
+        grouped_of, codes_of, planes_of, git_of = {}, {}, {}, {}
+        rz_of, n_of = {}, {}
+
+        def load_x(half):
+            x_sb = x_pool.tile([P, PAIR, K], BF16)
+            nc.sync.dma_start(out=x_sb[:], in_=x_rows[:, half * PAIR : (half + 1) * PAIR, :])
+            x_of[half] = x_sb
+
+        def load_gh_h(rnd):
+            tiles = slice(rnd * 2 * PAIR, (rnd + 1) * 2 * PAIR)
+            gh_sb = gh_pool.tile([P, 2 * PAIR, GATES], BF16)
             nc.sync.dma_start(out=gh_sb[:], in_=gh_rows[:, tiles, :])
-            h_sb = loads.tile([P, ROUND_TILES, HIDDEN], BF16)
+            h_sb = gh_pool.tile([P, 2 * PAIR, HIDDEN], BF16)
             nc.sync.dma_start(out=h_sb[:], in_=h_rows[:, tiles, :])
-            return x_sb, gh_sb, h_sb
+            gh_of[rnd], h_of[rnd] = gh_sb, h_sb
 
-        first_loads = load_round(0)
+        load_x(0)
+        load_x(1)
 
-        ident = const.tile([P, P], F32)
-        make_identity(nc, ident[:])
+        bias_rows = const.tile([P, P], BF16)
+        nc.vector.memset(bias_rows[:], 0.0)
+        nc.sync.dma_start(out=bias_rows[0:GATE_TILES, :], in_=b_ih0.rearrange("(j c) -> j c", c=P))
 
         w_codes = const.tile([P, PASSES, 2 * GATES], U8, align_bytes=64)
         nc.sync.dma_start(
@@ -77,9 +99,115 @@ def tile_grucellstack_pa_t_kernel(tc, x, h0, gh0, w_words, w_scales, b_ih0, out)
                 in_=w_scales[:, 4 * quad : 4 * quad + 4, :].rearrange("g r n -> r g n").bitcast(I32),
             )
 
-        bias_rows = const.tile([P, P], BF16)
-        nc.vector.memset(bias_rows[:], 0.0)
-        nc.sync.dma_start(out=bias_rows[0:GATE_TILES, :], in_=b_ih0.rearrange("(j c) -> j c", c=P))
+        load_x(2)
+        load_x(3)
+        load_gh_h(0)
+        for half in range(4, X_LEAD + X_LOAD_LEAD):
+            load_x(half)
+
+        ident = const.tile([P, P], F32)
+        make_identity(nc, ident[:])
+
+        def transpose_x(half):
+            rnd, side = divmod(half, 2)
+            if side == 0:
+                grouped_of[rnd] = quant.tile([P, PASSES, ROUND_ROWS, PACK], BF16, align_bytes=64, name="grouped")
+                codes_of[rnd] = quant.tile([P, PASSES, ROUND_ROWS], U32, align_bytes=64, name="x_codes")
+                planes_of[rnd] = quant.tile([P, PASSES, ROUND_ROWS], U8, align_bytes=64, name="x_planes")
+            grouped, x_codes, x_planes = grouped_of[rnd], codes_of[rnd], planes_of[rnd]
+            grouped_words = grouped[:].bitcast(F32)
+            for s in range(PAIR):
+                x_words = x_of[half][:, s, :].bitcast(F32)
+                xt = psum_xt.tile([P, PASSES, 2, P], F32)
+                for g in range(PASSES):
+                    for u in range(2):
+                        words = slice(g * PASS_WORDS + u, (g + 1) * PASS_WORDS, 2)
+                        nc.tensor.transpose(xt[:, g, u, :], x_words[:, words], ident[:])
+                first = side * HALF_ROWS + s * P
+                nc.scalar.copy(
+                    out=grouped_words[:, :, first : first + P, :],
+                    in_=xt[:].rearrange("p g u r -> p g r u"),
+                )
+            if side == 1:
+                nc.vector.quantize_mx(
+                    out=x_codes[:].rearrange("p g r -> p (g r)").bitcast(FP8X4),
+                    scales=x_planes[:].rearrange("p g r -> p (g r)"),
+                    in_=grouped[:].rearrange("p g r t -> p (g r t)"),
+                )
+
+        def project(half):
+            rnd, side = divmod(half, 2)
+            if side == 0:
+                git_of[rnd] = git_pool.tile([P, GATE_TILES, ROUND_ROWS], F32, name="gi_t")
+            for j in range(side * GATE_TILES // 2, (side + 1) * GATE_TILES // 2):
+                acc = psum_git.tile([P, ROUND_ROWS], F32)
+                for g in range(PASSES):
+                    nc.tensor.matmul_mx(
+                        out=acc[:],
+                        lhsT=w_codes[:, g, 2 * P * j : 2 * P * (j + 1)].bitcast(FP4X4),
+                        lhsT_scale=w_planes[:, g, P * j : P * (j + 1)],
+                        rhs=codes_of[rnd][:, g, :].bitcast(FP8X4),
+                        rhs_scale=planes_of[rnd][:, g, :],
+                        start=(g == 0),
+                        stop=(g == PASSES - 1),
+                    )
+                nc.scalar.activation(
+                    out=git_of[rnd][:, j, :], in_=acc[:], func=ACT.Identity, bias=bias_col[:, j : j + 1]
+                )
+
+        def add_gh(half):
+            rnd, side = divmod(half, 2)
+            rz = work.tile([P, PAIR, 2 * HIDDEN], F32)
+            for s in range(PAIR):
+                tile_in_round = side * PAIR + s
+                rows = slice(tile_in_round * P, (tile_in_round + 1) * P)
+                gi_rz = psum_rz.tile([P, 2 * HIDDEN], F32)
+                for j in range(RZ_TILES):
+                    nc.tensor.transpose(gi_rz[:, j * P : (j + 1) * P], git_of[rnd][:, j, rows], ident[:])
+                nc.vector.tensor_tensor(
+                    out=rz[:, s, :], in0=gi_rz[:], in1=gh_of[rnd][:, tile_in_round, 0 : 2 * HIDDEN], op=ALU.add
+                )
+            rz_of[half] = rz
+
+        def sigmoid_rz(half):
+            nc.scalar.activation(out=rz_of[half][:], in_=rz_of[half][:], func=ACT.Sigmoid)
+
+        def candidate(half):
+            rnd, side = divmod(half, 2)
+            pair = slice(side * PAIR, (side + 1) * PAIR)
+            gi_n = psum_n.tile([P, PAIR, HIDDEN], F32, tag="gi_n")
+            for s in range(PAIR):
+                rows = slice((side * PAIR + s) * P, (side * PAIR + s + 1) * P)
+                for j in range(RZ_TILES, GATE_TILES):
+                    cols = slice((j - RZ_TILES) * P, (j - RZ_TILES + 1) * P)
+                    nc.tensor.transpose(gi_n[:, s, cols], git_of[rnd][:, j, rows], ident[:])
+            n_gate = work.tile([P, PAIR, HIDDEN], F32)
+            nc.vector.tensor_tensor(
+                out=n_gate[:], in0=rz_of[half][:, :, 0:HIDDEN], in1=gh_of[rnd][:, pair, 2 * HIDDEN : GATES], op=ALU.mult
+            )
+            nc.vector.tensor_tensor(out=n_gate[:], in0=gi_n[:], in1=n_gate[:], op=ALU.add)
+            n_of[half] = n_gate
+
+        def tanh_n(half):
+            nc.scalar.activation(out=n_of[half][:], in_=n_of[half][:], func=ACT.Tanh)
+
+        def blend(half):
+            rnd, side = divmod(half, 2)
+            pair = slice(side * PAIR, (side + 1) * PAIR)
+            n_gate = n_of[half]
+            diff = work.tile([P, PAIR, HIDDEN], F32)
+            nc.vector.tensor_tensor(out=diff[:], in0=h_of[rnd][:, pair, :], in1=n_gate[:], op=ALU.subtract)
+            nc.vector.tensor_tensor(out=diff[:], in0=rz_of[half][:, :, HIDDEN : 2 * HIDDEN], in1=diff[:], op=ALU.mult)
+            out_sb = work.tile([P, PAIR, HIDDEN], F32)
+            nc.vector.tensor_tensor(out=out_sb[:], in0=diff[:], in1=n_gate[:], op=ALU.add)
+            nc.sync.dma_start(out=out_rows[:, half * PAIR : (half + 1) * PAIR, :], in_=out_sb[:])
+
+        def exists(half):
+            return 0 <= half < HALVES
+
+        for half in range(X_LEAD):
+            transpose_x(half)
+
         bias_rows_f32 = const.tile([P, P], F32)
         nc.vector.tensor_copy(out=bias_rows_f32[:], in_=bias_rows[:])
         bias_ps = psum_n.tile([P, PAIR, HIDDEN], F32, tag="gi_n")
@@ -87,84 +215,23 @@ def tile_grucellstack_pa_t_kernel(tc, x, h0, gh0, w_words, w_scales, b_ih0, out)
         bias_col = const.tile([P, GATE_TILES], F32)
         nc.vector.tensor_copy(out=bias_col[:], in_=bias_ps[:, 0, 0:GATE_TILES])
 
-        def quantise_round(x_sb):
-            grouped = quant.tile([P, PASSES, ROUND_ROWS, PACK], BF16, align_bytes=64)
-            grouped_words = grouped[:].bitcast(F32)
-            for i in range(ROUND_TILES):
-                x_words = x_sb[:, i, :].bitcast(F32)
-                xt = psum_xt.tile([P, PASSES, 2, P], F32)
-                for g in range(PASSES):
-                    for u in range(2):
-                        first = g * (WORDS // PASSES) + u
-                        last = (g + 1) * (WORDS // PASSES)
-                        nc.tensor.transpose(xt[:, g, u, :], x_words[:, first:last:2], ident[:])
-                nc.scalar.copy(
-                    out=grouped_words[:, :, i * P : (i + 1) * P, :],
-                    in_=xt[:].rearrange("p g u r -> p g r u"),
-                )
-            x_codes = quant.tile([P, PASSES, ROUND_ROWS], U32, align_bytes=64)
-            x_planes = quant.tile([P, PASSES, ROUND_ROWS], U8, align_bytes=64)
-            nc.vector.quantize_mx(
-                out=x_codes[:].rearrange("p g r -> p (g r)").bitcast(FP8X4),
-                scales=x_planes[:].rearrange("p g r -> p (g r)"),
-                in_=grouped[:].rearrange("p g r t -> p (g r t)"),
-            )
-            return x_codes, x_planes
-
-        def project_round(x_codes, x_planes):
-            gi_t = quant.tile([P, GATE_TILES, ROUND_ROWS], F32)
-            for j in range(GATE_TILES):
-                acc = psum_git.tile([P, ROUND_ROWS], F32)
-                for g in range(PASSES):
-                    nc.tensor.matmul_mx(
-                        out=acc[:],
-                        lhsT=w_codes[:, g, 2 * P * j : 2 * P * (j + 1)].bitcast(FP4X4),
-                        lhsT_scale=w_planes[:, g, P * j : P * (j + 1)],
-                        rhs=x_codes[:, g, :].bitcast(FP8X4),
-                        rhs_scale=x_planes[:, g, :],
-                        start=(g == 0),
-                        stop=(g == PASSES - 1),
-                    )
-                nc.scalar.activation(
-                    out=gi_t[:, j, :], in_=acc[:], func=ACT.Identity, bias=bias_col[:, j : j + 1]
-                )
-            return gi_t
-
-        def gates_round(rnd, gi_t, gh_sb, h_sb):
-            out_sb = work.tile([P, ROUND_TILES, HIDDEN], F32)
-            for first in range(0, ROUND_TILES, PAIR):
-                pair = slice(first, first + PAIR)
-                rz = work.tile([P, PAIR, 2 * HIDDEN], F32)
-                gi_n = psum_n.tile([P, PAIR, HIDDEN], F32, tag="gi_n")
-                for s in range(PAIR):
-                    rows = slice((first + s) * P, (first + s + 1) * P)
-                    gi_rz = psum_rz.tile([P, 2 * HIDDEN], F32)
-                    for j in range(RZ_TILES):
-                        nc.tensor.transpose(gi_rz[:, j * P : (j + 1) * P], gi_t[:, j, rows], ident[:])
-                    for j in range(RZ_TILES, GATE_TILES):
-                        cols = slice((j - RZ_TILES) * P, (j - RZ_TILES + 1) * P)
-                        nc.tensor.transpose(gi_n[:, s, cols], gi_t[:, j, rows], ident[:])
-                    nc.vector.tensor_tensor(
-                        out=rz[:, s, :], in0=gi_rz[:], in1=gh_sb[:, first + s, 0 : 2 * HIDDEN], op=ALU.add
-                    )
-                nc.scalar.activation(out=rz[:], in_=rz[:], func=ACT.Sigmoid)
-                r_gate = rz[:, :, 0:HIDDEN]
-                z_gate = rz[:, :, HIDDEN : 2 * HIDDEN]
-                n_gate = work.tile([P, PAIR, HIDDEN], F32)
-                nc.vector.tensor_tensor(
-                    out=n_gate[:], in0=r_gate, in1=gh_sb[:, pair, 2 * HIDDEN : GATES], op=ALU.mult
-                )
-                nc.vector.tensor_tensor(out=n_gate[:], in0=gi_n[:], in1=n_gate[:], op=ALU.add)
-                nc.scalar.activation(out=n_gate[:], in_=n_gate[:], func=ACT.Tanh)
-                diff = work.tile([P, PAIR, HIDDEN], F32)
-                nc.vector.tensor_tensor(out=diff[:], in0=h_sb[:, pair, :], in1=n_gate[:], op=ALU.subtract)
-                nc.vector.tensor_tensor(out=diff[:], in0=z_gate, in1=diff[:], op=ALU.mult)
-                nc.vector.tensor_tensor(out=out_sb[:, pair, :], in0=diff[:], in1=n_gate[:], op=ALU.add)
-            tiles = slice(rnd * ROUND_TILES, (rnd + 1) * ROUND_TILES)
-            nc.sync.dma_start(out=out_rows[:, tiles, :], in_=out_sb[:])
-
-        for rnd in range(ROUNDS):
-            x_sb, gh_sb, h_sb = first_loads if rnd == 0 else load_round(rnd)
-            x_codes, x_planes = quantise_round(x_sb)
-            gi_t = project_round(x_codes, x_planes)
-            gates_round(rnd, gi_t, gh_sb, h_sb)
+        for step in range(HALVES + BLEND_LAG):
+            if exists(step + X_LEAD + X_LOAD_LEAD):
+                load_x(step + X_LEAD + X_LOAD_LEAD)
+            first_use = step + GH_LOAD_LEAD - ADD_LAG
+            if exists(first_use) and first_use % 2 == 0:
+                load_gh_h(first_use // 2)
+            if exists(step - TANH_LAG):
+                tanh_n(step - TANH_LAG)
+            if exists(step - SIGMOID_LAG):
+                sigmoid_rz(step - SIGMOID_LAG)
+            if exists(step - BLEND_LAG):
+                blend(step - BLEND_LAG)
+            if exists(step - ADD_LAG):
+                add_gh(step - ADD_LAG)
+            if exists(step - CANDIDATE_LAG):
+                candidate(step - CANDIDATE_LAG)
+            if exists(step + X_LEAD):
+                transpose_x(step + X_LEAD)
+            if exists(step):
+                project(step)

@@ -61,7 +61,6 @@ def tile_grucellstack_pa_t_kernel(tc, x, h0, gh0, w_words, w_scales, b_ih0, out)
         psum_git = ctx.enter_context(tc.psum_pool(name="psum_git", bufs=3))
         psum_rz = ctx.enter_context(tc.psum_pool(name="psum_rz", bufs=2))
         psum_n = ctx.enter_context(tc.psum_pool(name="psum_n", bufs=1))
-        ctx.enter_context(tc.manual_schedule())
 
         x_of, gh_of, h_of = {}, {}, {}
         grouped_of, codes_of, planes_of, git_of = {}, {}, {}, {}

@@ -64,7 +64,7 @@ def tile_grucellstack_pa_t_kernel(tc, x, h0, gh0, w_words, w_scales, b_ih0, out)
 
         x_of, gh_of, h_of = {}, {}, {}
         grouped_of, codes_of, planes_of, git_of = {}, {}, {}, {}
-        rz_of, n_of = {}, {}
+        rz_of, n_of, gi_n_of, diff_of = {}, {}, {}, {}
 
         def load_x(half):
             x_sb = x_pool.tile([P, PAIR, K], BF16)
@@ -154,24 +154,23 @@ def tile_grucellstack_pa_t_kernel(tc, x, h0, gh0, w_words, w_scales, b_ih0, out)
                     out=git_of[rnd][:, j, :], in_=acc[:], func=ACT.Identity, bias=bias_col[:, j : j + 1]
                 )
 
-        def add_gh(half):
+        def add_gh(half, s):
             rnd, side = divmod(half, 2)
-            rz = work.tile([P, PAIR, 2 * HIDDEN], F32)
-            for s in range(PAIR):
-                tile_in_round = side * PAIR + s
-                rows = slice(tile_in_round * P, (tile_in_round + 1) * P)
-                gi_rz = psum_rz.tile([P, 2 * HIDDEN], F32)
-                for j in range(RZ_TILES):
-                    nc.tensor.transpose(gi_rz[:, j * P : (j + 1) * P], git_of[rnd][:, j, rows], ident[:])
-                nc.vector.tensor_tensor(
-                    out=rz[:, s, :], in0=gi_rz[:], in1=gh_of[rnd][:, tile_in_round, 0 : 2 * HIDDEN], op=ALU.add
-                )
-            rz_of[half] = rz
+            if s == 0:
+                rz_of[half] = work.tile([P, PAIR, 2 * HIDDEN], F32, name="rz")
+            tile_in_round = side * PAIR + s
+            rows = slice(tile_in_round * P, (tile_in_round + 1) * P)
+            gi_rz = psum_rz.tile([P, 2 * HIDDEN], F32)
+            for j in range(RZ_TILES):
+                nc.tensor.transpose(gi_rz[:, j * P : (j + 1) * P], git_of[rnd][:, j, rows], ident[:])
+            nc.vector.tensor_tensor(
+                out=rz_of[half][:, s, :], in0=gi_rz[:], in1=gh_of[rnd][:, tile_in_round, 0 : 2 * HIDDEN], op=ALU.add
+            )
 
         def sigmoid_rz(half):
             nc.scalar.activation(out=rz_of[half][:], in_=rz_of[half][:], func=ACT.Sigmoid)
 
-        def candidate(half):
+        def candidate_product(half):
             rnd, side = divmod(half, 2)
             pair = slice(side * PAIR, (side + 1) * PAIR)
             gi_n = psum_n.tile([P, PAIR, HIDDEN], F32, tag="gi_n")
@@ -184,21 +183,28 @@ def tile_grucellstack_pa_t_kernel(tc, x, h0, gh0, w_words, w_scales, b_ih0, out)
             nc.vector.tensor_tensor(
                 out=n_gate[:], in0=rz_of[half][:, :, 0:HIDDEN], in1=gh_of[rnd][:, pair, 2 * HIDDEN : GATES], op=ALU.mult
             )
-            nc.vector.tensor_tensor(out=n_gate[:], in0=gi_n[:], in1=n_gate[:], op=ALU.add)
-            n_of[half] = n_gate
+            n_of[half], gi_n_of[half] = n_gate, gi_n
+
+        def candidate_sum(half):
+            nc.vector.tensor_tensor(out=n_of[half][:], in0=gi_n_of[half][:], in1=n_of[half][:], op=ALU.add)
 
         def tanh_n(half):
             nc.scalar.activation(out=n_of[half][:], in_=n_of[half][:], func=ACT.Tanh)
 
-        def blend(half):
+        def blend_diff(half):
             rnd, side = divmod(half, 2)
             pair = slice(side * PAIR, (side + 1) * PAIR)
-            n_gate = n_of[half]
             diff = work.tile([P, PAIR, HIDDEN], F32)
-            nc.vector.tensor_tensor(out=diff[:], in0=h_of[rnd][:, pair, :], in1=n_gate[:], op=ALU.subtract)
+            nc.vector.tensor_tensor(out=diff[:], in0=h_of[rnd][:, pair, :], in1=n_of[half][:], op=ALU.subtract)
+            diff_of[half] = diff
+
+        def blend_scale(half):
+            diff = diff_of[half]
             nc.vector.tensor_tensor(out=diff[:], in0=rz_of[half][:, :, HIDDEN : 2 * HIDDEN], in1=diff[:], op=ALU.mult)
+
+        def blend_sum(half):
             out_sb = work.tile([P, PAIR, HIDDEN], F32)
-            nc.vector.tensor_tensor(out=out_sb[:], in0=diff[:], in1=n_gate[:], op=ALU.add)
+            nc.vector.tensor_tensor(out=out_sb[:], in0=diff_of[half][:], in1=n_of[half][:], op=ALU.add)
             nc.sync.dma_start(out=out_rows[:, half * PAIR : (half + 1) * PAIR, :], in_=out_sb[:])
 
         def exists(half):
@@ -225,11 +231,19 @@ def tile_grucellstack_pa_t_kernel(tc, x, h0, gh0, w_words, w_scales, b_ih0, out)
             if exists(step - SIGMOID_LAG):
                 sigmoid_rz(step - SIGMOID_LAG)
             if exists(step - BLEND_LAG):
-                blend(step - BLEND_LAG)
+                blend_diff(step - BLEND_LAG)
             if exists(step - ADD_LAG):
-                add_gh(step - ADD_LAG)
+                add_gh(step - ADD_LAG, 0)
+            if exists(step - BLEND_LAG):
+                blend_scale(step - BLEND_LAG)
+            if exists(step - ADD_LAG):
+                add_gh(step - ADD_LAG, 1)
             if exists(step - CANDIDATE_LAG):
-                candidate(step - CANDIDATE_LAG)
+                candidate_product(step - CANDIDATE_LAG)
+            if exists(step - BLEND_LAG):
+                blend_sum(step - BLEND_LAG)
+            if exists(step - CANDIDATE_LAG):
+                candidate_sum(step - CANDIDATE_LAG)
             if exists(step + X_LEAD):
                 transpose_x(step + X_LEAD)
             if exists(step):

@@ -32,7 +32,6 @@ HALVES = 2 * ROUNDS
 
 X_LEAD = 2
 ADD_LAG = 2
-SIGMOID_LAG = 3
 CANDIDATE_LAG = 3
 TANH_LAG = 4
 BLEND_LAG = 5
@@ -106,6 +105,8 @@ def tile_grucellstack_pa_t_kernel(tc, x, h0, gh0, w_words, w_scales, b_ih0, out)
 
         ident = const.tile([P, P], F32)
         make_identity(nc, ident[:])
+        ident_bf16 = const.tile([P, P], BF16)
+        make_identity(nc, ident_bf16[:])
 
         def transpose_x(half):
             rnd, side = divmod(half, 2)
@@ -123,7 +124,8 @@ def tile_grucellstack_pa_t_kernel(tc, x, h0, gh0, w_words, w_scales, b_ih0, out)
                         words = slice(g * PASS_WORDS + u, (g + 1) * PASS_WORDS, 2)
                         nc.tensor.transpose(xt[:, g, u, :], x_words[:, words], ident[:])
                 first = side * HALF_ROWS + s * P
-                nc.scalar.copy(
+                copy_out = nc.scalar.copy if s == 0 else nc.vector.tensor_copy
+                copy_out(
                     out=grouped_words[:, :, first : first + P, :],
                     in_=xt[:].rearrange("p g u r -> p g r u"),
                 )
@@ -161,14 +163,19 @@ def tile_grucellstack_pa_t_kernel(tc, x, h0, gh0, w_words, w_scales, b_ih0, out)
             tile_in_round = side * PAIR + s
             rows = slice(tile_in_round * P, (tile_in_round + 1) * P)
             gi_rz = psum_rz.tile([P, 2 * HIDDEN], F32)
-            for j in range(RZ_TILES):
-                nc.tensor.transpose(gi_rz[:, j * P : (j + 1) * P], git_of[rnd][:, j, rows], ident[:])
-            nc.vector.tensor_tensor(
-                out=rz_of[half][:, s, :], in0=gi_rz[:], in1=gh_of[rnd][:, tile_in_round, 0 : 2 * HIDDEN], op=ALU.add
+            nc.tensor.matmul(
+                gi_rz[:], lhsT=ident_bf16[:], rhs=gh_of[rnd][:, tile_in_round, 0 : 2 * HIDDEN], start=True, stop=False
             )
-
-        def sigmoid_rz(half):
-            nc.scalar.activation(out=rz_of[half][:], in_=rz_of[half][:], func=ACT.Sigmoid)
+            for j in range(RZ_TILES):
+                nc.tensor.matmul(
+                    gi_rz[:, j * P : (j + 1) * P],
+                    lhsT=git_of[rnd][:, j, rows],
+                    rhs=ident[:],
+                    is_transpose=True,
+                    start=False,
+                    stop=(j == RZ_TILES - 1),
+                )
+            nc.scalar.activation(out=rz_of[half][:, s, :], in_=gi_rz[:], func=ACT.Sigmoid)
 
         def candidate_product(half):
             rnd, side = divmod(half, 2)
@@ -228,8 +235,6 @@ def tile_grucellstack_pa_t_kernel(tc, x, h0, gh0, w_words, w_scales, b_ih0, out)
                 load_gh_h(first_use // 2)
             if exists(step - TANH_LAG):
                 tanh_n(step - TANH_LAG)
-            if exists(step - SIGMOID_LAG):
-                sigmoid_rz(step - SIGMOID_LAG)
             if exists(step - BLEND_LAG):
                 blend_diff(step - BLEND_LAG)
             if exists(step - ADD_LAG):

@@ -63,7 +63,7 @@ def tile_grucellstack_pa_t_kernel(tc, x, h0, gh0, w_words, w_scales, b_ih0, out)
 
         x_of, gh_of, h_of = {}, {}, {}
         grouped_of, codes_of, planes_of, git_of = {}, {}, {}, {}
-        rz_of, n_of, gi_n_of, diff_of = {}, {}, {}, {}
+        rz_of, n_of, gi_n_of, diff_of, acc_of, gi_rz_of = {}, {}, {}, {}, {}, {}
 
         def load_x(half):
             x_sb = x_pool.tile([P, PAIR, K], BF16)
@@ -108,53 +108,61 @@ def tile_grucellstack_pa_t_kernel(tc, x, h0, gh0, w_words, w_scales, b_ih0, out)
         ident_bf16 = const.tile([P, P], BF16)
         make_identity(nc, ident_bf16[:])
 
-        def transpose_x(half):
+        def transpose_x(half, s):
             rnd, side = divmod(half, 2)
-            if side == 0:
+            if side == 0 and s == 0:
                 grouped_of[rnd] = quant.tile([P, PASSES, ROUND_ROWS, PACK], BF16, align_bytes=64, name="grouped")
                 codes_of[rnd] = quant.tile([P, PASSES, ROUND_ROWS], U32, align_bytes=64, name="x_codes")
                 planes_of[rnd] = quant.tile([P, PASSES, ROUND_ROWS], U8, align_bytes=64, name="x_planes")
-            grouped, x_codes, x_planes = grouped_of[rnd], codes_of[rnd], planes_of[rnd]
-            grouped_words = grouped[:].bitcast(F32)
-            for s in range(PAIR):
-                x_words = x_of[half][:, s, :].bitcast(F32)
-                xt = psum_xt.tile([P, PASSES, 2, P], F32)
-                for g in range(PASSES):
-                    for u in range(2):
-                        words = slice(g * PASS_WORDS + u, (g + 1) * PASS_WORDS, 2)
-                        nc.tensor.transpose(xt[:, g, u, :], x_words[:, words], ident[:])
-                first = side * HALF_ROWS + s * P
-                copy_out = nc.scalar.copy if s == 0 else nc.vector.tensor_copy
-                copy_out(
-                    out=grouped_words[:, :, first : first + P, :],
-                    in_=xt[:].rearrange("p g u r -> p g r u"),
-                )
-            if side == 1:
+            grouped_words = grouped_of[rnd][:].bitcast(F32)
+            x_words = x_of[half][:, s, :].bitcast(F32)
+            xt = psum_xt.tile([P, PASSES, 2, P], F32)
+            for g in range(PASSES):
+                for u in range(2):
+                    words = slice(g * PASS_WORDS + u, (g + 1) * PASS_WORDS, 2)
+                    nc.tensor.transpose(xt[:, g, u, :], x_words[:, words], ident[:])
+            first = side * HALF_ROWS + s * P
+            copy_out = nc.scalar.copy if s == 0 else nc.vector.tensor_copy
+            copy_out(
+                out=grouped_words[:, :, first : first + P, :],
+                in_=xt[:].rearrange("p g u r -> p g r u"),
+            )
+            if side == 1 and s == PAIR - 1:
                 nc.vector.quantize_mx(
-                    out=x_codes[:].rearrange("p g r -> p (g r)").bitcast(FP8X4),
-                    scales=x_planes[:].rearrange("p g r -> p (g r)"),
-                    in_=grouped[:].rearrange("p g r t -> p (g r t)"),
+                    out=codes_of[rnd][:].rearrange("p g r -> p (g r)").bitcast(FP8X4),
+                    scales=planes_of[rnd][:].rearrange("p g r -> p (g r)"),
+                    in_=grouped_of[rnd][:].rearrange("p g r t -> p (g r t)"),
                 )
 
-        def project(half):
-            rnd, side = divmod(half, 2)
-            if side == 0:
+        def project_pass(step, number):
+            rnd, side = divmod(step, 2)
+            if side == 0 and number == 0:
                 git_of[rnd] = git_pool.tile([P, GATE_TILES, ROUND_ROWS], F32, name="gi_t")
-            for j in range(side * GATE_TILES // 2, (side + 1) * GATE_TILES // 2):
-                acc = psum_git.tile([P, ROUND_ROWS], F32)
-                for g in range(PASSES):
-                    nc.tensor.matmul_mx(
-                        out=acc[:],
-                        lhsT=w_codes[:, g, 2 * P * j : 2 * P * (j + 1)].bitcast(FP4X4),
-                        lhsT_scale=w_planes[:, g, P * j : P * (j + 1)],
-                        rhs=codes_of[rnd][:, g, :].bitcast(FP8X4),
-                        rhs_scale=planes_of[rnd][:, g, :],
-                        start=(g == 0),
-                        stop=(g == PASSES - 1),
-                    )
+            j, g = side * GATE_TILES // 2 + number // PASSES, number % PASSES
+            if g == 0:
+                acc_of[step] = psum_git.tile([P, ROUND_ROWS], F32, name="acc")
+            acc = acc_of[step]
+            nc.tensor.matmul_mx(
+                out=acc[:],
+                lhsT=w_codes[:, g, 2 * P * j : 2 * P * (j + 1)].bitcast(FP4X4),
+                lhsT_scale=w_planes[:, g, P * j : P * (j + 1)],
+                rhs=codes_of[rnd][:, g, :].bitcast(FP8X4),
+                rhs_scale=planes_of[rnd][:, g, :],
+                start=(g == 0),
+                stop=(g == PASSES - 1),
+            )
+            if g == PASSES - 1:
                 nc.scalar.activation(
                     out=git_of[rnd][:, j, :], in_=acc[:], func=ACT.Identity, bias=bias_col[:, j : j + 1]
                 )
+
+        def open_rz(half, s):
+            rnd, side = divmod(half, 2)
+            gi_rz = psum_rz.tile([P, 2 * HIDDEN], F32)
+            nc.tensor.matmul(
+                gi_rz[:], lhsT=ident_bf16[:], rhs=gh_of[rnd][:, side * PAIR + s, 0 : 2 * HIDDEN], start=True, stop=False
+            )
+            gi_rz_of[half, s] = gi_rz
 
         def add_gh(half, s):
             rnd, side = divmod(half, 2)
@@ -162,10 +170,7 @@ def tile_grucellstack_pa_t_kernel(tc, x, h0, gh0, w_words, w_scales, b_ih0, out)
                 rz_of[half] = work.tile([P, PAIR, 2 * HIDDEN], F32, name="rz")
             tile_in_round = side * PAIR + s
             rows = slice(tile_in_round * P, (tile_in_round + 1) * P)
-            gi_rz = psum_rz.tile([P, 2 * HIDDEN], F32)
-            nc.tensor.matmul(
-                gi_rz[:], lhsT=ident_bf16[:], rhs=gh_of[rnd][:, tile_in_round, 0 : 2 * HIDDEN], start=True, stop=False
-            )
+            gi_rz = gi_rz_of[half, s]
             for j in range(RZ_TILES):
                 nc.tensor.matmul(
                     gi_rz[:, j * P : (j + 1) * P],
@@ -218,7 +223,8 @@ def tile_grucellstack_pa_t_kernel(tc, x, h0, gh0, w_words, w_scales, b_ih0, out)
             return 0 <= half < HALVES
 
         for half in range(X_LEAD):
-            transpose_x(half)
+            for s in range(PAIR):
+                transpose_x(half, s)
 
         bias_rows_f32 = const.tile([P, P], F32)
         nc.vector.tensor_copy(out=bias_rows_f32[:], in_=bias_rows[:])
@@ -227,29 +233,37 @@ def tile_grucellstack_pa_t_kernel(tc, x, h0, gh0, w_words, w_scales, b_ih0, out)
         bias_col = const.tile([P, GATE_TILES], F32)
         nc.vector.tensor_copy(out=bias_col[:], in_=bias_ps[:, 0, 0:GATE_TILES])
 
-        for step in range(HALVES + BLEND_LAG):
-            if exists(step + X_LEAD + X_LOAD_LEAD):
-                load_x(step + X_LEAD + X_LOAD_LEAD)
-            first_use = step + GH_LOAD_LEAD - ADD_LAG
-            if exists(first_use) and first_use % 2 == 0:
-                load_gh_h(first_use // 2)
-            if exists(step - TANH_LAG):
-                tanh_n(step - TANH_LAG)
-            if exists(step - BLEND_LAG):
-                blend_diff(step - BLEND_LAG)
-            if exists(step - ADD_LAG):
-                add_gh(step - ADD_LAG, 0)
-            if exists(step - BLEND_LAG):
-                blend_scale(step - BLEND_LAG)
-            if exists(step - ADD_LAG):
-                add_gh(step - ADD_LAG, 1)
-            if exists(step - CANDIDATE_LAG):
-                candidate_product(step - CANDIDATE_LAG)
-            if exists(step - BLEND_LAG):
-                blend_sum(step - BLEND_LAG)
-            if exists(step - CANDIDATE_LAG):
-                candidate_sum(step - CANDIDATE_LAG)
-            if exists(step + X_LEAD):
-                transpose_x(step + X_LEAD)
-            if exists(step):
-                project(step)
+        with tc.manual_schedule(engines={mybir.EngineType.PE}):
+            for step in range(HALVES + BLEND_LAG):
+                if exists(step + X_LEAD + X_LOAD_LEAD):
+                    load_x(step + X_LEAD + X_LOAD_LEAD)
+                first_use = step + GH_LOAD_LEAD - ADD_LAG
+                if exists(first_use) and first_use % 2 == 0:
+                    load_gh_h(first_use // 2)
+                if exists(step - TANH_LAG):
+                    tanh_n(step - TANH_LAG)
+                if exists(step - ADD_LAG):
+                    open_rz(step - ADD_LAG, 0)
+                if exists(step - ADD_LAG):
+                    open_rz(step - ADD_LAG, 1)
+                if exists(step - BLEND_LAG):
+                    blend_diff(step - BLEND_LAG)
+                if exists(step - ADD_LAG):
+                    add_gh(step - ADD_LAG, 0)
+                if exists(step - BLEND_LAG):
+                    blend_scale(step - BLEND_LAG)
+                if exists(step - ADD_LAG):
+                    add_gh(step - ADD_LAG, 1)
+                if exists(step - CANDIDATE_LAG):
+                    candidate_product(step - CANDIDATE_LAG)
+                if exists(step - BLEND_LAG):
+                    blend_sum(step - BLEND_LAG)
+                if exists(step - CANDIDATE_LAG):
+                    candidate_sum(step - CANDIDATE_LAG)
+                if exists(step + X_LEAD):
+                    transpose_x(step + X_LEAD, 0)
+                if exists(step + X_LEAD):
+                    transpose_x(step + X_LEAD, 1)
+                if exists(step):
+                    for number in range(0, 6):
+                        project_pass(step, number)

@@ -56,10 +56,7 @@ def tile_grucellstack_pa_t_kernel(tc, x, h0, gh0, w_words, w_scales, b_ih0, out)
         quant = ctx.enter_context(tc.tile_pool(name="quant", bufs=2))
         git_pool = ctx.enter_context(tc.tile_pool(name="git_pool", bufs=3))
         work = ctx.enter_context(tc.tile_pool(name="work", bufs=BLEND_LAG - ADD_LAG + 1))
-        psum_xt = ctx.enter_context(tc.psum_pool(name="psum_xt", bufs=2))
-        psum_git = ctx.enter_context(tc.psum_pool(name="psum_git", bufs=3))
-        psum_rz = ctx.enter_context(tc.psum_pool(name="psum_rz", bufs=2))
-        psum_n = ctx.enter_context(tc.psum_pool(name="psum_n", bufs=1))
+        psum = ctx.enter_context(tc.psum_pool(name="psum", bufs=8))
 
         x_of, gh_of, h_of = {}, {}, {}
         grouped_of, codes_of, planes_of, git_of = {}, {}, {}, {}
@@ -77,6 +74,10 @@ def tile_grucellstack_pa_t_kernel(tc, x, h0, gh0, w_words, w_scales, b_ih0, out)
             h_sb = gh_pool.tile([P, 2 * PAIR, HIDDEN], BF16)
             nc.sync.dma_start(out=h_sb[:], in_=h_rows[:, tiles, :])
             gh_of[rnd], h_of[rnd] = gh_sb, h_sb
+
+        warm = const.tile([P, 1], F32)
+        nc.vector.memset(warm[:], 0.0)
+        nc.scalar.activation(out=warm[:], in_=warm[:], func=ACT.Sigmoid)
 
         load_x(0)
         load_x(1)
@@ -116,7 +117,7 @@ def tile_grucellstack_pa_t_kernel(tc, x, h0, gh0, w_words, w_scales, b_ih0, out)
                 planes_of[rnd] = quant.tile([P, PASSES, ROUND_ROWS], U8, align_bytes=64, name="x_planes")
             grouped_words = grouped_of[rnd][:].bitcast(F32)
             x_words = x_of[half][:, s, :].bitcast(F32)
-            xt = psum_xt.tile([P, PASSES, 2, P], F32)
+            xt = psum.tile([P, PASSES, 2, P], F32, tag="bank")
             for g in range(PASSES):
                 for u in range(2):
                     words = slice(g * PASS_WORDS + u, (g + 1) * PASS_WORDS, 2)
@@ -140,7 +141,7 @@ def tile_grucellstack_pa_t_kernel(tc, x, h0, gh0, w_words, w_scales, b_ih0, out)
                 git_of[rnd] = git_pool.tile([P, GATE_TILES, ROUND_ROWS], F32, name="gi_t")
             j, g = side * GATE_TILES // 2 + number // PASSES, number % PASSES
             if g == 0:
-                acc_of[step] = psum_git.tile([P, ROUND_ROWS], F32, name="acc")
+                acc_of[step] = psum.tile([P, ROUND_ROWS], F32, name="acc", tag="bank")
             acc = acc_of[step]
             nc.tensor.matmul_mx(
                 out=acc[:],
@@ -158,7 +159,7 @@ def tile_grucellstack_pa_t_kernel(tc, x, h0, gh0, w_words, w_scales, b_ih0, out)
 
         def open_rz(half, s):
             rnd, side = divmod(half, 2)
-            gi_rz = psum_rz.tile([P, 2 * HIDDEN], F32)
+            gi_rz = psum.tile([P, 2 * HIDDEN], F32, tag="bank")
             nc.tensor.matmul(
                 gi_rz[:], lhsT=ident_bf16[:], rhs=gh_of[rnd][:, side * PAIR + s, 0 : 2 * HIDDEN], start=True, stop=False
             )
@@ -185,7 +186,7 @@ def tile_grucellstack_pa_t_kernel(tc, x, h0, gh0, w_words, w_scales, b_ih0, out)
         def candidate_product(half):
             rnd, side = divmod(half, 2)
             pair = slice(side * PAIR, (side + 1) * PAIR)
-            gi_n = psum_n.tile([P, PAIR, HIDDEN], F32, tag="gi_n")
+            gi_n = psum.tile([P, PAIR, HIDDEN], F32, tag="bank")
             for s in range(PAIR):
                 rows = slice((side * PAIR + s) * P, (side * PAIR + s + 1) * P)
                 for j in range(RZ_TILES, GATE_TILES):
@@ -228,7 +229,7 @@ def tile_grucellstack_pa_t_kernel(tc, x, h0, gh0, w_words, w_scales, b_ih0, out)
 
         bias_rows_f32 = const.tile([P, P], F32)
         nc.vector.tensor_copy(out=bias_rows_f32[:], in_=bias_rows[:])
-        bias_ps = psum_n.tile([P, PAIR, HIDDEN], F32, tag="gi_n")
+        bias_ps = psum.tile([P, PAIR, HIDDEN], F32, tag="bank")
         nc.tensor.transpose(bias_ps[:, 0, 0:P], bias_rows_f32[:], ident[:])
         bias_col = const.tile([P, GATE_TILES], F32)
         nc.vector.tensor_copy(out=bias_col[:], in_=bias_ps[:, 0, 0:GATE_TILES])

@@ -64,7 +64,11 @@ def tile_grucellstack_pa_t_kernel(tc, x, h0, gh0, w_words, w_scales, b_ih0, out)
 
         def load_x(half):
             x_sb = x_pool.tile([P, PAIR, K], BF16)
-            nc.sync.dma_start(out=x_sb[:], in_=x_rows[:, half * PAIR : (half + 1) * PAIR, :])
+            if half < 2:
+                for s in range(PAIR):
+                    nc.sync.dma_start(out=x_sb[:, s, :], in_=x_rows[:, half * PAIR + s, :])
+            else:
+                nc.sync.dma_start(out=x_sb[:], in_=x_rows[:, half * PAIR : (half + 1) * PAIR, :])
             x_of[half] = x_sb
 
         def load_gh_h(rnd):
@@ -234,7 +238,7 @@ def tile_grucellstack_pa_t_kernel(tc, x, h0, gh0, w_words, w_scales, b_ih0, out)
         bias_col = const.tile([P, GATE_TILES], F32)
         nc.vector.tensor_copy(out=bias_col[:], in_=bias_ps[:, 0, 0:GATE_TILES])
 
-        with tc.manual_schedule(engines={mybir.EngineType.PE}):
+        with tc.manual_schedule(engines={mybir.EngineType.PE, mybir.EngineType.Activation, mybir.EngineType.DVE}):
             for step in range(HALVES + BLEND_LAG):
                 if exists(step + X_LEAD + X_LOAD_LEAD):
                     load_x(step + X_LEAD + X_LOAD_LEAD)

@@ -51,11 +51,11 @@ def tile_grucellstack_pa_t_kernel(tc, x, h0, gh0, w_words, w_scales, b_ih0, out)
 
     with ExitStack() as ctx:
         const = ctx.enter_context(tc.tile_pool(name="const", bufs=1))
-        x_pool = ctx.enter_context(tc.tile_pool(name="x_pool", bufs=X_LOAD_LEAD + 2))
+        x_pool = ctx.enter_context(tc.tile_pool(name="x_pool", bufs=X_LEAD + X_LOAD_LEAD + 1))
         gh_pool = ctx.enter_context(tc.tile_pool(name="gh_pool", bufs=(GH_LOAD_LEAD + BLEND_LAG) // 2 + 1))
-        quant = ctx.enter_context(tc.tile_pool(name="quant", bufs=2))
+        quant = ctx.enter_context(tc.tile_pool(name="quant", bufs=3))
         git_pool = ctx.enter_context(tc.tile_pool(name="git_pool", bufs=3))
-        work = ctx.enter_context(tc.tile_pool(name="work", bufs=BLEND_LAG - ADD_LAG + 1))
+        work = ctx.enter_context(tc.tile_pool(name="work", bufs=4))
         psum = ctx.enter_context(tc.psum_pool(name="psum", bufs=8))
 
         x_of, gh_of, h_of = {}, {}, {}
@@ -187,20 +187,24 @@ def tile_grucellstack_pa_t_kernel(tc, x, h0, gh0, w_words, w_scales, b_ih0, out)
                 )
             nc.scalar.activation(out=rz_of[half][:, s, :], in_=gi_rz[:], func=ACT.Sigmoid)
 
-        def candidate_product(half):
+        def transpose_gi_n(half):
             rnd, side = divmod(half, 2)
-            pair = slice(side * PAIR, (side + 1) * PAIR)
             gi_n = psum.tile([P, PAIR, HIDDEN], F32, tag="bank")
             for s in range(PAIR):
                 rows = slice((side * PAIR + s) * P, (side * PAIR + s + 1) * P)
                 for j in range(RZ_TILES, GATE_TILES):
                     cols = slice((j - RZ_TILES) * P, (j - RZ_TILES + 1) * P)
                     nc.tensor.transpose(gi_n[:, s, cols], git_of[rnd][:, j, rows], ident[:])
+            gi_n_of[half] = gi_n
+
+        def candidate_product(half):
+            rnd, side = divmod(half, 2)
+            pair = slice(side * PAIR, (side + 1) * PAIR)
             n_gate = work.tile([P, PAIR, HIDDEN], F32)
             nc.vector.tensor_tensor(
                 out=n_gate[:], in0=rz_of[half][:, :, 0:HIDDEN], in1=gh_of[rnd][:, pair, 2 * HIDDEN : GATES], op=ALU.mult
             )
-            n_of[half], gi_n_of[half] = n_gate, gi_n
+            n_of[half] = n_gate
 
         def candidate_sum(half):
             nc.vector.tensor_tensor(out=n_of[half][:], in0=gi_n_of[half][:], in1=n_of[half][:], op=ALU.add)
@@ -255,16 +259,18 @@ def tile_grucellstack_pa_t_kernel(tc, x, h0, gh0, w_words, w_scales, b_ih0, out)
                     blend_diff(step - BLEND_LAG)
                 if exists(step - ADD_LAG):
                     add_gh(step - ADD_LAG, 0)
+                if exists(step - CANDIDATE_LAG):
+                    transpose_gi_n(step - CANDIDATE_LAG)
+                if exists(step - CANDIDATE_LAG):
+                    candidate_product(step - CANDIDATE_LAG)
                 if exists(step - BLEND_LAG):
                     blend_scale(step - BLEND_LAG)
                 if exists(step - ADD_LAG):
                     add_gh(step - ADD_LAG, 1)
                 if exists(step - CANDIDATE_LAG):
-                    candidate_product(step - CANDIDATE_LAG)
+                    candidate_sum(step - CANDIDATE_LAG)
                 if exists(step - BLEND_LAG):
                     blend_sum(step - BLEND_LAG)
-                if exists(step - CANDIDATE_LAG):
-                    candidate_sum(step - CANDIDATE_LAG)
                 if exists(step + X_LEAD):
                     transpose_x(step + X_LEAD, 0)
                 if exists(step + X_LEAD):

@@ -38,6 +38,8 @@ BLEND_LAG = 5
 X_LOAD_LEAD = 4
 GH_LOAD_LEAD = 4
 
+LAST_STEP = HALVES + BLEND_LAG - 2
+
 FLOPS = 2 * ROWS * K * GATES
 
 
@@ -132,12 +134,13 @@ def tile_grucellstack_pa_t_kernel(tc, x, h0, gh0, w_words, w_scales, b_ih0, out)
                 out=grouped_words[:, :, first : first + P, :],
                 in_=xt[:].rearrange("p g u r -> p g r u"),
             )
-            if side == 1 and s == PAIR - 1:
-                nc.vector.quantize_mx(
-                    out=codes_of[rnd][:].rearrange("p g r -> p (g r)").bitcast(FP8X4),
-                    scales=planes_of[rnd][:].rearrange("p g r -> p (g r)"),
-                    in_=grouped_of[rnd][:].rearrange("p g r t -> p (g r t)"),
-                )
+
+        def quantise(rnd):
+            nc.vector.quantize_mx(
+                out=codes_of[rnd][:].rearrange("p g r -> p (g r)").bitcast(FP8X4),
+                scales=planes_of[rnd][:].rearrange("p g r -> p (g r)"),
+                in_=grouped_of[rnd][:].rearrange("p g r t -> p (g r t)"),
+            )
 
         def project_pass(step, number):
             rnd, side = divmod(step, 2)
@@ -243,34 +246,37 @@ def tile_grucellstack_pa_t_kernel(tc, x, h0, gh0, w_words, w_scales, b_ih0, out)
         nc.vector.tensor_copy(out=bias_col[:], in_=bias_ps[:, 0, 0:GATE_TILES])
 
         with tc.manual_schedule(engines={mybir.EngineType.PE, mybir.EngineType.Activation, mybir.EngineType.DVE}):
-            for step in range(HALVES + BLEND_LAG):
+            for step in range(LAST_STEP + 1):
                 if exists(step + X_LEAD + X_LOAD_LEAD):
                     load_x(step + X_LEAD + X_LOAD_LEAD)
                 first_use = step + GH_LOAD_LEAD - ADD_LAG
                 if exists(first_use) and first_use % 2 == 0:
                     load_gh_h(first_use // 2)
+                blends = [half for half in range(step - BLEND_LAG, HALVES if step == LAST_STEP else step - BLEND_LAG + 1) if exists(half)]
                 if exists(step - TANH_LAG):
                     tanh_n(step - TANH_LAG)
                 if exists(step - ADD_LAG):
                     open_rz(step - ADD_LAG, 0)
                 if exists(step - ADD_LAG):
                     open_rz(step - ADD_LAG, 1)
-                if exists(step - BLEND_LAG):
-                    blend_diff(step - BLEND_LAG)
+                for half in blends:
+                    blend_diff(half)
+                if exists(step) and step % 2 == 0:
+                    quantise(step // 2)
                 if exists(step - ADD_LAG):
                     add_gh(step - ADD_LAG, 0)
                 if exists(step - CANDIDATE_LAG):
                     transpose_gi_n(step - CANDIDATE_LAG)
                 if exists(step - CANDIDATE_LAG):
                     candidate_product(step - CANDIDATE_LAG)
-                if exists(step - BLEND_LAG):
-                    blend_scale(step - BLEND_LAG)
+                for half in blends:
+                    blend_scale(half)
                 if exists(step - ADD_LAG):
                     add_gh(step - ADD_LAG, 1)
                 if exists(step - CANDIDATE_LAG):
                     candidate_sum(step - CANDIDATE_LAG)
-                if exists(step - BLEND_LAG):
-                    blend_sum(step - BLEND_LAG)
+                for half in blends:
+                    blend_sum(half)
                 if exists(step + X_LEAD):
                     transpose_x(step + X_LEAD, 0)
                 if exists(step + X_LEAD):

@@ -32,6 +32,7 @@ HALVES = 2 * ROUNDS
 
 X_LEAD = 2
 ADD_LAG = 2
+PRE_LAG = 1
 CANDIDATE_LAG = 3
 TANH_LAG = 4
 BLEND_LAG = 5
@@ -62,7 +63,13 @@ def tile_grucellstack_pa_t_kernel(tc, x, h0, gh0, w_words, w_scales, b_ih0, out)
 
         x_of, gh_of, h_of = {}, {}, {}
         grouped_of, codes_of, planes_of, git_of = {}, {}, {}, {}
+        pre_of, keep_of, new_of = {}, {}, {}
         rz_of, n_of, gi_n_of, diff_of, acc_of, gi_rz_of = {}, {}, {}, {}, {}, {}
+
+        bn_rows = const.tile([P, PAIR, HIDDEN], BF16)
+        nc.vector.memset(bn_rows[:], 0.0)
+        ones = const.tile([P, P], BF16)
+        nc.vector.memset(ones[:], 1.0)
 
         def load_x(half):
             x_sb = x_pool.tile([P, PAIR, K], BF16)
@@ -91,6 +98,11 @@ def tile_grucellstack_pa_t_kernel(tc, x, h0, gh0, w_words, w_scales, b_ih0, out)
         bias_rows = const.tile([P, P], BF16)
         nc.vector.memset(bias_rows[:], 0.0)
         nc.sync.dma_start(out=bias_rows[0:GATE_TILES, :], in_=b_ih0.rearrange("(j c) -> j c", c=P))
+
+        for s in range(PAIR):
+            nc.sync.dma_start(
+                out=bn_rows[0:1, s, :], in_=b_ih0[2 * HIDDEN : GATES].rearrange("(o c) -> o c", o=1)
+            )
 
         w_codes = const.tile([P, PASSES, 2 * GATES], U8, align_bytes=64)
         nc.sync.dma_start(
@@ -129,8 +141,7 @@ def tile_grucellstack_pa_t_kernel(tc, x, h0, gh0, w_words, w_scales, b_ih0, out)
                     words = slice(g * PASS_WORDS + u, (g + 1) * PASS_WORDS, 2)
                     nc.tensor.transpose(xt[:, g, u, :], x_words[:, words], ident[:])
             first = side * HALF_ROWS + s * P
-            copy_out = nc.scalar.copy if s == 0 else nc.vector.tensor_copy
-            copy_out(
+            nc.scalar.copy(
                 out=grouped_words[:, :, first : first + P, :],
                 in_=xt[:].rearrange("p g u r -> p g r u"),
             )
@@ -142,11 +153,11 @@ def tile_grucellstack_pa_t_kernel(tc, x, h0, gh0, w_words, w_scales, b_ih0, out)
                 in_=grouped_of[rnd][:].rearrange("p g r t -> p (g r t)"),
             )
 
-        def project_pass(step, number):
+        def project_rz(step, number):
             rnd, side = divmod(step, 2)
             if side == 0 and number == 0:
-                git_of[rnd] = git_pool.tile([P, GATE_TILES, ROUND_ROWS], F32, name="gi_t")
-            j, g = side * GATE_TILES // 2 + number // PASSES, number % PASSES
+                git_of[rnd] = git_pool.tile([P, RZ_TILES, ROUND_ROWS], F32, name="gi_t")
+            j, g = side * RZ_TILES // 2 + number // PASSES, number % PASSES
             if g == 0:
                 acc_of[step] = psum.tile([P, ROUND_ROWS], F32, name="acc", tag="bank")
             acc = acc_of[step]
@@ -163,6 +174,30 @@ def tile_grucellstack_pa_t_kernel(tc, x, h0, gh0, w_words, w_scales, b_ih0, out)
                 nc.scalar.activation(
                     out=git_of[rnd][:, j, :], in_=acc[:], func=ACT.Identity, bias=bias_col[:, j : j + 1]
                 )
+
+        def project_n(half):
+            rnd, side = divmod(half, 2)
+            gi_n = psum.tile([P, PAIR, HIDDEN], F32, tag="bank")
+            for s in range(PAIR):
+                rows = slice((side * PAIR + s) * P, (side * PAIR + s + 1) * P)
+                for c in range(HIDDEN // P):
+                    j = RZ_TILES + c
+                    for g in range(PASSES):
+                        nc.tensor.matmul_mx(
+                            out=gi_n[:, s, c * P : (c + 1) * P],
+                            lhsT=codes_of[rnd][:, g, rows].bitcast(FP8X4),
+                            lhsT_scale=planes_of[rnd][:, g, rows],
+                            rhs=w_codes[:, g, 2 * P * j : 2 * P * (j + 1)].bitcast(FP4X4),
+                            rhs_scale=w_planes[:, g, P * j : P * (j + 1)],
+                            start=(g == 0),
+                            stop=(g == PASSES - 1),
+                        )
+            gi_n_of[half] = gi_n
+
+        def bias_n(half):
+            pre_n = work.tile([P, PAIR, HIDDEN], F32)
+            nc.vector.tensor_tensor(out=pre_n[:], in0=gi_n_of[half][:], in1=b_n[:], op=ALU.add)
+            pre_of[half] = pre_n
 
         def open_rz(half, s):
             rnd, side = divmod(half, 2)
@@ -190,16 +225,6 @@ def tile_grucellstack_pa_t_kernel(tc, x, h0, gh0, w_words, w_scales, b_ih0, out)
                 )
             nc.scalar.activation(out=rz_of[half][:, s, :], in_=gi_rz[:], func=ACT.Sigmoid)
 
-        def transpose_gi_n(half):
-            rnd, side = divmod(half, 2)
-            gi_n = psum.tile([P, PAIR, HIDDEN], F32, tag="bank")
-            for s in range(PAIR):
-                rows = slice((side * PAIR + s) * P, (side * PAIR + s + 1) * P)
-                for j in range(RZ_TILES, GATE_TILES):
-                    cols = slice((j - RZ_TILES) * P, (j - RZ_TILES + 1) * P)
-                    nc.tensor.transpose(gi_n[:, s, cols], git_of[rnd][:, j, rows], ident[:])
-            gi_n_of[half] = gi_n
-
         def candidate_product(half):
             rnd, side = divmod(half, 2)
             pair = slice(side * PAIR, (side + 1) * PAIR)
@@ -210,25 +235,32 @@ def tile_grucellstack_pa_t_kernel(tc, x, h0, gh0, w_words, w_scales, b_ih0, out)
             n_of[half] = n_gate
 
         def candidate_sum(half):
-            nc.vector.tensor_tensor(out=n_of[half][:], in0=gi_n_of[half][:], in1=n_of[half][:], op=ALU.add)
+            nc.vector.tensor_tensor(out=n_of[half][:], in0=pre_of[half][:], in1=n_of[half][:], op=ALU.add)
 
         def tanh_n(half):
             nc.scalar.activation(out=n_of[half][:], in_=n_of[half][:], func=ACT.Tanh)
 
-        def blend_diff(half):
+        def blend_keep(half):
             rnd, side = divmod(half, 2)
             pair = slice(side * PAIR, (side + 1) * PAIR)
-            diff = work.tile([P, PAIR, HIDDEN], F32)
-            nc.vector.tensor_tensor(out=diff[:], in0=h_of[rnd][:, pair, :], in1=n_of[half][:], op=ALU.subtract)
-            diff_of[half] = diff
+            keep = work.tile([P, PAIR, HIDDEN], F32)
+            nc.vector.tensor_tensor(
+                out=keep[:], in0=rz_of[half][:, :, HIDDEN : 2 * HIDDEN], in1=h_of[rnd][:, pair, :], op=ALU.mult
+            )
+            keep_of[half] = keep
 
-        def blend_scale(half):
-            diff = diff_of[half]
-            nc.vector.tensor_tensor(out=diff[:], in0=rz_of[half][:, :, HIDDEN : 2 * HIDDEN], in1=diff[:], op=ALU.mult)
+        def blend_new(half):
+            n_gate = n_of[half]
+            new = work.tile([P, PAIR, HIDDEN], F32)
+            nc.vector.scalar_tensor_tensor(
+                out=new[:], in0=rz_of[half][:, :, HIDDEN : 2 * HIDDEN], scalar=1.0, in1=n_gate[:],
+                op0=ALU.subtract, op1=ALU.mult,
+            )
+            new_of[half] = new
 
         def blend_sum(half):
             out_sb = work.tile([P, PAIR, HIDDEN], F32)
-            nc.vector.tensor_tensor(out=out_sb[:], in0=diff_of[half][:], in1=n_of[half][:], op=ALU.add)
+            nc.vector.tensor_tensor(out=out_sb[:], in0=keep_of[half][:], in1=new_of[half][:], op=ALU.subtract)
             nc.sync.dma_start(out=out_rows[:, half * PAIR : (half + 1) * PAIR, :], in_=out_sb[:])
 
         def exists(half):
@@ -245,6 +277,11 @@ def tile_grucellstack_pa_t_kernel(tc, x, h0, gh0, w_words, w_scales, b_ih0, out)
         bias_col = const.tile([P, GATE_TILES], F32)
         nc.vector.tensor_copy(out=bias_col[:], in_=bias_ps[:, 0, 0:GATE_TILES])
 
+        b_n_ps = psum.tile([P, PAIR, HIDDEN], F32, tag="bank")
+        nc.tensor.matmul(b_n_ps[:], lhsT=ones[:], rhs=bn_rows[:], start=True, stop=True)
+        b_n = const.tile([P, PAIR, HIDDEN], F32)
+        nc.vector.tensor_copy(out=b_n[:], in_=b_n_ps[:])
+
         with tc.manual_schedule(engines={mybir.EngineType.PE, mybir.EngineType.Activation, mybir.EngineType.DVE}):
             for step in range(LAST_STEP + 1):
                 if exists(step + X_LEAD + X_LOAD_LEAD):
@@ -255,32 +292,31 @@ def tile_grucellstack_pa_t_kernel(tc, x, h0, gh0, w_words, w_scales, b_ih0, out)
                 blends = [half for half in range(step - BLEND_LAG, HALVES if step == LAST_STEP else step - BLEND_LAG + 1) if exists(half)]
                 if exists(step - TANH_LAG):
                     tanh_n(step - TANH_LAG)
-                if exists(step - ADD_LAG):
-                    open_rz(step - ADD_LAG, 0)
-                if exists(step - ADD_LAG):
-                    open_rz(step - ADD_LAG, 1)
+                for s in range(PAIR):
+                    if exists(step - ADD_LAG):
+                        open_rz(step - ADD_LAG, s)
                 for half in blends:
-                    blend_diff(half)
+                    blend_new(half)
                 if exists(step) and step % 2 == 0:
                     quantise(step // 2)
                 if exists(step - ADD_LAG):
                     add_gh(step - ADD_LAG, 0)
-                if exists(step - CANDIDATE_LAG):
-                    transpose_gi_n(step - CANDIDATE_LAG)
+                if exists(step - PRE_LAG):
+                    bias_n(step - PRE_LAG)
                 if exists(step - CANDIDATE_LAG):
                     candidate_product(step - CANDIDATE_LAG)
                 for half in blends:
-                    blend_scale(half)
+                    blend_sum(half)
                 if exists(step - ADD_LAG):
                     add_gh(step - ADD_LAG, 1)
                 if exists(step - CANDIDATE_LAG):
                     candidate_sum(step - CANDIDATE_LAG)
-                for half in blends:
-                    blend_sum(half)
-                if exists(step + X_LEAD):
-                    transpose_x(step + X_LEAD, 0)
-                if exists(step + X_LEAD):
-                    transpose_x(step + X_LEAD, 1)
+                if exists(step - CANDIDATE_LAG):
+                    blend_keep(step - CANDIDATE_LAG)
+                for s in range(PAIR):
+                    if exists(step + X_LEAD):
+                        transpose_x(step + X_LEAD, s)
                 if exists(step):
-                    for number in range(0, 6):
-                        project_pass(step, number)
+                    for number in range(4):
+                        project_rz(step, number)
+                    project_n(step)

@@ -30,16 +30,17 @@ ROUND_ROWS = 2 * HALF_ROWS
 ROUNDS = ROWS // ROUND_ROWS
 HALVES = 2 * ROUNDS
 
-X_LEAD = 2
-ADD_LAG = 2
+X_LEAD = 1
+ADD_LAG = 1
 PRE_LAG = 1
-CANDIDATE_LAG = 3
+X_HEAD = 3
+CANDIDATE_LAG = 2
 TANH_LAG = 4
-BLEND_LAG = 5
-X_LOAD_LEAD = 4
-GH_LOAD_LEAD = 4
+BLEND_LAG = 3
+X_LOAD_LEAD = 5
+GH_LOAD_LEAD = 2
 
-LAST_STEP = HALVES + BLEND_LAG - 2
+LAST_STEP = HALVES + BLEND_LAG - 1
 
 FLOPS = 2 * ROWS * K * GATES
 
@@ -56,8 +57,8 @@ def tile_grucellstack_pa_t_kernel(tc, x, h0, gh0, w_words, w_scales, b_ih0, out)
         const = ctx.enter_context(tc.tile_pool(name="const", bufs=1))
         x_pool = ctx.enter_context(tc.tile_pool(name="x_pool", bufs=X_LEAD + X_LOAD_LEAD + 1))
         gh_pool = ctx.enter_context(tc.tile_pool(name="gh_pool", bufs=(GH_LOAD_LEAD + BLEND_LAG) // 2 + 1))
-        quant = ctx.enter_context(tc.tile_pool(name="quant", bufs=3))
-        git_pool = ctx.enter_context(tc.tile_pool(name="git_pool", bufs=3))
+        quant = ctx.enter_context(tc.tile_pool(name="quant", bufs=4))
+        git_pool = ctx.enter_context(tc.tile_pool(name="git_pool", bufs=4))
         work = ctx.enter_context(tc.tile_pool(name="work", bufs=4))
         psum = ctx.enter_context(tc.psum_pool(name="psum", bufs=8))
 
@@ -65,11 +66,6 @@ def tile_grucellstack_pa_t_kernel(tc, x, h0, gh0, w_words, w_scales, b_ih0, out)
         grouped_of, codes_of, planes_of, git_of = {}, {}, {}, {}
         pre_of, keep_of, new_of = {}, {}, {}
         rz_of, n_of, gi_n_of, diff_of, acc_of, gi_rz_of = {}, {}, {}, {}, {}, {}
-
-        bn_rows = const.tile([P, PAIR, HIDDEN], BF16)
-        nc.vector.memset(bn_rows[:], 0.0)
-        ones = const.tile([P, P], BF16)
-        nc.vector.memset(ones[:], 1.0)
 
         def load_x(half):
             x_sb = x_pool.tile([P, PAIR, K], BF16)
@@ -80,29 +76,30 @@ def tile_grucellstack_pa_t_kernel(tc, x, h0, gh0, w_words, w_scales, b_ih0, out)
                 nc.sync.dma_start(out=x_sb[:], in_=x_rows[:, half * PAIR : (half + 1) * PAIR, :])
             x_of[half] = x_sb
 
-        def load_gh_h(rnd):
-            tiles = slice(rnd * 2 * PAIR, (rnd + 1) * 2 * PAIR)
+        def load_gh_h(first, count):
+            tiles = slice(first * PAIR, (first + count) * PAIR)
             gh_sb = gh_pool.tile([P, 2 * PAIR, GATES], BF16)
-            nc.sync.dma_start(out=gh_sb[:], in_=gh_rows[:, tiles, :])
+            nc.sync.dma_start(out=gh_sb[:, 0 : count * PAIR, :], in_=gh_rows[:, tiles, :])
             h_sb = gh_pool.tile([P, 2 * PAIR, HIDDEN], BF16)
-            nc.sync.dma_start(out=h_sb[:], in_=h_rows[:, tiles, :])
-            gh_of[rnd], h_of[rnd] = gh_sb, h_sb
+            nc.sync.dma_start(out=h_sb[:, 0 : count * PAIR, :], in_=h_rows[:, tiles, :])
+            for i in range(count):
+                gh_of[first + i] = gh_sb[:, i * PAIR : (i + 1) * PAIR, :]
+                h_of[first + i] = h_sb[:, i * PAIR : (i + 1) * PAIR, :]
 
         warm = const.tile([P, 1], F32)
         nc.vector.memset(warm[:], 0.0)
         nc.scalar.activation(out=warm[:], in_=warm[:], func=ACT.Sigmoid)
 
-        load_x(0)
-        load_x(1)
-
         bias_rows = const.tile([P, P], BF16)
         nc.vector.memset(bias_rows[:], 0.0)
-        nc.sync.dma_start(out=bias_rows[0:GATE_TILES, :], in_=b_ih0.rearrange("(j c) -> j c", c=P))
+        nc.scalar.dma_start(out=bias_rows[0:GATE_TILES, :], in_=b_ih0.rearrange("(j c) -> j c", c=P))
+        bn_row = const.tile([P, HIDDEN], BF16)
+        nc.vector.memset(bn_row[:], 0.0)
+        nc.scalar.dma_start(out=bn_row[0:1, :], in_=b_ih0[2 * HIDDEN : GATES].rearrange("(o c) -> o c", o=1))
+        ones = const.tile([P, P], BF16)
+        nc.vector.memset(ones[:], 1.0)
 
-        for s in range(PAIR):
-            nc.sync.dma_start(
-                out=bn_rows[0:1, s, :], in_=b_ih0[2 * HIDDEN : GATES].rearrange("(o c) -> o c", o=1)
-            )
+        load_x(0)
 
         w_codes = const.tile([P, PASSES, 2 * GATES], U8, align_bytes=64)
         nc.sync.dma_start(
@@ -116,10 +113,11 @@ def tile_grucellstack_pa_t_kernel(tc, x, h0, gh0, w_words, w_scales, b_ih0, out)
                 in_=w_scales[:, 4 * quad : 4 * quad + 4, :].rearrange("g r n -> r g n").bitcast(I32),
             )
 
+        load_x(1)
+        load_gh_h(0, 1)
         load_x(2)
-        load_x(3)
-        load_gh_h(0)
-        for half in range(4, X_LEAD + X_LOAD_LEAD):
+        load_gh_h(1, 1)
+        for half in range(3, X_LEAD + X_LOAD_LEAD):
             load_x(half)
 
         ident = const.tile([P, P], F32)
@@ -128,65 +126,65 @@ def tile_grucellstack_pa_t_kernel(tc, x, h0, gh0, w_words, w_scales, b_ih0, out)
         make_identity(nc, ident_bf16[:])
 
         def transpose_x(half, s):
-            rnd, side = divmod(half, 2)
-            if side == 0 and s == 0:
-                grouped_of[rnd] = quant.tile([P, PASSES, ROUND_ROWS, PACK], BF16, align_bytes=64, name="grouped")
-                codes_of[rnd] = quant.tile([P, PASSES, ROUND_ROWS], U32, align_bytes=64, name="x_codes")
-                planes_of[rnd] = quant.tile([P, PASSES, ROUND_ROWS], U8, align_bytes=64, name="x_planes")
-            grouped_words = grouped_of[rnd][:].bitcast(F32)
+            if s == 0:
+                grouped_of[half] = quant.tile([P, PASSES, HALF_ROWS, PACK], BF16, align_bytes=64, name="grouped")
+            grouped_words = grouped_of[half][:].bitcast(F32)
             x_words = x_of[half][:, s, :].bitcast(F32)
             xt = psum.tile([P, PASSES, 2, P], F32, tag="bank")
             for g in range(PASSES):
                 for u in range(2):
                     words = slice(g * PASS_WORDS + u, (g + 1) * PASS_WORDS, 2)
                     nc.tensor.transpose(xt[:, g, u, :], x_words[:, words], ident[:])
-            first = side * HALF_ROWS + s * P
-            nc.scalar.copy(
-                out=grouped_words[:, :, first : first + P, :],
+            copy_out = nc.vector.tensor_copy if half < X_HEAD and s == 1 else nc.scalar.copy
+            copy_out(
+                out=grouped_words[:, :, s * P : (s + 1) * P, :],
                 in_=xt[:].rearrange("p g u r -> p g r u"),
             )
 
-        def quantise(rnd):
+        def quantise(half):
+            codes_of[half] = quant.tile([P, PASSES, HALF_ROWS], U32, align_bytes=64, name="x_codes")
+            planes_of[half] = quant.tile([P, PASSES, HALF_ROWS], U8, align_bytes=64, name="x_planes")
             nc.vector.quantize_mx(
-                out=codes_of[rnd][:].rearrange("p g r -> p (g r)").bitcast(FP8X4),
-                scales=planes_of[rnd][:].rearrange("p g r -> p (g r)"),
-                in_=grouped_of[rnd][:].rearrange("p g r t -> p (g r t)"),
+                out=codes_of[half][:].rearrange("p g r -> p (g r)").bitcast(FP8X4),
+                scales=planes_of[half][:].rearrange("p g r -> p (g r)"),
+                in_=grouped_of[half][:].rearrange("p g r t -> p (g r t)"),
             )
 
-        def project_rz(step, number):
-            rnd, side = divmod(step, 2)
-            if side == 0 and number == 0:
-                git_of[rnd] = git_pool.tile([P, RZ_TILES, ROUND_ROWS], F32, name="gi_t")
-            j, g = side * RZ_TILES // 2 + number // PASSES, number % PASSES
-            if g == 0:
-                acc_of[step] = psum.tile([P, ROUND_ROWS], F32, name="acc", tag="bank")
-            acc = acc_of[step]
-            nc.tensor.matmul_mx(
-                out=acc[:],
-                lhsT=w_codes[:, g, 2 * P * j : 2 * P * (j + 1)].bitcast(FP4X4),
-                lhsT_scale=w_planes[:, g, P * j : P * (j + 1)],
-                rhs=codes_of[rnd][:, g, :].bitcast(FP8X4),
-                rhs_scale=planes_of[rnd][:, g, :],
-                start=(g == 0),
-                stop=(g == PASSES - 1),
-            )
-            if g == PASSES - 1:
-                nc.scalar.activation(
-                    out=git_of[rnd][:, j, :], in_=acc[:], func=ACT.Identity, bias=bias_col[:, j : j + 1]
-                )
+        def project_rz(half):
+            git_of[half] = git_pool.tile([P, RZ_TILES, HALF_ROWS], F32, name="gi_t")
+            for first in range(0, RZ_TILES, 2):
+                acc = psum.tile([P, 2, HALF_ROWS], F32, tag="bank")
+                for i in range(2):
+                    j = first + i
+                    for s in range(PAIR):
+                        rows = slice(s * P, (s + 1) * P)
+                        for g in range(PASSES):
+                            nc.tensor.matmul_mx(
+                                out=acc[:, i, rows],
+                                lhsT=w_codes[:, g, 2 * P * j : 2 * P * (j + 1)].bitcast(FP4X4),
+                                lhsT_scale=w_planes[:, g, P * j : P * (j + 1)],
+                                rhs=codes_of[half][:, g, rows].bitcast(FP8X4),
+                                rhs_scale=planes_of[half][:, g, rows],
+                                start=(g == 0),
+                                stop=(g == PASSES - 1),
+                            )
+                for i in range(2):
+                    j = first + i
+                    nc.scalar.activation(
+                        out=git_of[half][:, j, :], in_=acc[:, i, :], func=ACT.Identity, bias=bias_col[:, j : j + 1]
+                    )
 
         def project_n(half):
-            rnd, side = divmod(half, 2)
             gi_n = psum.tile([P, PAIR, HIDDEN], F32, tag="bank")
             for s in range(PAIR):
-                rows = slice((side * PAIR + s) * P, (side * PAIR + s + 1) * P)
+                rows = slice(s * P, (s + 1) * P)
                 for c in range(HIDDEN // P):
                     j = RZ_TILES + c
                     for g in range(PASSES):
                         nc.tensor.matmul_mx(
                             out=gi_n[:, s, c * P : (c + 1) * P],
-                            lhsT=codes_of[rnd][:, g, rows].bitcast(FP8X4),
-                            lhsT_scale=planes_of[rnd][:, g, rows],
+                            lhsT=codes_of[half][:, g, rows].bitcast(FP8X4),
+                            lhsT_scale=planes_of[half][:, g, rows],
                             rhs=w_codes[:, g, 2 * P * j : 2 * P * (j + 1)].bitcast(FP4X4),
                             rhs_scale=w_planes[:, g, P * j : P * (j + 1)],
                             start=(g == 0),
@@ -200,24 +198,21 @@ def tile_grucellstack_pa_t_kernel(tc, x, h0, gh0, w_words, w_scales, b_ih0, out)
             pre_of[half] = pre_n
 
         def open_rz(half, s):
-            rnd, side = divmod(half, 2)
             gi_rz = psum.tile([P, 2 * HIDDEN], F32, tag="bank")
             nc.tensor.matmul(
-                gi_rz[:], lhsT=ident_bf16[:], rhs=gh_of[rnd][:, side * PAIR + s, 0 : 2 * HIDDEN], start=True, stop=False
+                gi_rz[:], lhsT=ident_bf16[:], rhs=gh_of[half][:, s, 0 : 2 * HIDDEN], start=True, stop=False
             )
             gi_rz_of[half, s] = gi_rz
 
         def add_gh(half, s):
-            rnd, side = divmod(half, 2)
             if s == 0:
                 rz_of[half] = work.tile([P, PAIR, 2 * HIDDEN], F32, name="rz")
-            tile_in_round = side * PAIR + s
-            rows = slice(tile_in_round * P, (tile_in_round + 1) * P)
+            rows = slice(s * P, (s + 1) * P)
             gi_rz = gi_rz_of[half, s]
             for j in range(RZ_TILES):
                 nc.tensor.matmul(
                     gi_rz[:, j * P : (j + 1) * P],
-                    lhsT=git_of[rnd][:, j, rows],
+                    lhsT=git_of[half][:, j, rows],
                     rhs=ident[:],
                     is_transpose=True,
                     start=False,
@@ -226,11 +221,9 @@ def tile_grucellstack_pa_t_kernel(tc, x, h0, gh0, w_words, w_scales, b_ih0, out)
             nc.scalar.activation(out=rz_of[half][:, s, :], in_=gi_rz[:], func=ACT.Sigmoid)
 
         def candidate_product(half):
-            rnd, side = divmod(half, 2)
-            pair = slice(side * PAIR, (side + 1) * PAIR)
             n_gate = work.tile([P, PAIR, HIDDEN], F32)
             nc.vector.tensor_tensor(
-                out=n_gate[:], in0=rz_of[half][:, :, 0:HIDDEN], in1=gh_of[rnd][:, pair, 2 * HIDDEN : GATES], op=ALU.mult
+                out=n_gate[:], in0=rz_of[half][:, :, 0:HIDDEN], in1=gh_of[half][:, :, 2 * HIDDEN : GATES], op=ALU.mult
             )
             n_of[half] = n_gate
 
@@ -241,11 +234,9 @@ def tile_grucellstack_pa_t_kernel(tc, x, h0, gh0, w_words, w_scales, b_ih0, out)
             nc.scalar.activation(out=n_of[half][:], in_=n_of[half][:], func=ACT.Tanh)
 
         def blend_keep(half):
-            rnd, side = divmod(half, 2)
-            pair = slice(side * PAIR, (side + 1) * PAIR)
             keep = work.tile([P, PAIR, HIDDEN], F32)
             nc.vector.tensor_tensor(
-                out=keep[:], in0=rz_of[half][:, :, HIDDEN : 2 * HIDDEN], in1=h_of[rnd][:, pair, :], op=ALU.mult
+                out=keep[:], in0=rz_of[half][:, :, HIDDEN : 2 * HIDDEN], in1=h_of[half], op=ALU.mult
             )
             keep_of[half] = keep
 
@@ -266,57 +257,57 @@ def tile_grucellstack_pa_t_kernel(tc, x, h0, gh0, w_words, w_scales, b_ih0, out)
         def exists(half):
             return 0 <= half < HALVES
 
-        for half in range(X_LEAD):
-            for s in range(PAIR):
-                transpose_x(half, s)
-
-        bias_rows_f32 = const.tile([P, P], F32)
-        nc.vector.tensor_copy(out=bias_rows_f32[:], in_=bias_rows[:])
-        bias_ps = psum.tile([P, PAIR, HIDDEN], F32, tag="bank")
-        nc.tensor.transpose(bias_ps[:, 0, 0:P], bias_rows_f32[:], ident[:])
-        bias_col = const.tile([P, GATE_TILES], F32)
-        nc.vector.tensor_copy(out=bias_col[:], in_=bias_ps[:, 0, 0:GATE_TILES])
-
-        b_n_ps = psum.tile([P, PAIR, HIDDEN], F32, tag="bank")
-        nc.tensor.matmul(b_n_ps[:], lhsT=ones[:], rhs=bn_rows[:], start=True, stop=True)
-        b_n = const.tile([P, PAIR, HIDDEN], F32)
-        nc.vector.tensor_copy(out=b_n[:], in_=b_n_ps[:])
-
         with tc.manual_schedule(engines={mybir.EngineType.PE, mybir.EngineType.Activation, mybir.EngineType.DVE}):
+            bias_rows_f32 = const.tile([P, P], F32)
+            nc.vector.tensor_copy(out=bias_rows_f32[:], in_=bias_rows[:])
+            for s in range(PAIR):
+                transpose_x(0, s)
+            bias_ps = psum.tile([P, PAIR, HIDDEN], F32, tag="bank")
+            nc.tensor.transpose(bias_ps[:, 0, 0:P], bias_rows_f32[:], ident[:])
+            quantise(0)
+            bias_col = const.tile([P, GATE_TILES], F32)
+            nc.vector.tensor_copy(out=bias_col[:], in_=bias_ps[:, 0, 0:GATE_TILES])
+            b_n_ps = psum.tile([P, PAIR, HIDDEN], F32, tag="bank")
+            for s in range(PAIR):
+                nc.tensor.matmul(b_n_ps[:, s, :], lhsT=ones[:], rhs=bn_row[:], start=True, stop=True)
+            b_n = const.tile([P, PAIR, HIDDEN], F32)
             for step in range(LAST_STEP + 1):
                 if exists(step + X_LEAD + X_LOAD_LEAD):
                     load_x(step + X_LEAD + X_LOAD_LEAD)
-                first_use = step + GH_LOAD_LEAD - ADD_LAG
+                first_use = step + GH_LOAD_LEAD
                 if exists(first_use) and first_use % 2 == 0:
-                    load_gh_h(first_use // 2)
-                blends = [half for half in range(step - BLEND_LAG, HALVES if step == LAST_STEP else step - BLEND_LAG + 1) if exists(half)]
-                if exists(step - TANH_LAG):
-                    tanh_n(step - TANH_LAG)
+                    load_gh_h(first_use, 2)
                 for s in range(PAIR):
                     if exists(step - ADD_LAG):
                         open_rz(step - ADD_LAG, s)
-                for half in blends:
-                    blend_new(half)
-                if exists(step) and step % 2 == 0:
-                    quantise(step // 2)
-                if exists(step - ADD_LAG):
-                    add_gh(step - ADD_LAG, 0)
+                if step >= HALVES and exists(step - ADD_LAG):
+                    for s in range(PAIR):
+                        add_gh(step - ADD_LAG, s)
+                if exists(step - CANDIDATE_LAG):
+                    candidate_product(step - CANDIDATE_LAG)
+                if exists(step - BLEND_LAG):
+                    blend_sum(step - BLEND_LAG)
+                if exists(step - CANDIDATE_LAG):
+                    candidate_sum(step - CANDIDATE_LAG)
+                if step > 0 and exists(step):
+                    quantise(step)
+                if exists(step - CANDIDATE_LAG):
+                    tanh_n(step - CANDIDATE_LAG)
                 if exists(step - PRE_LAG):
                     bias_n(step - PRE_LAG)
                 if exists(step - CANDIDATE_LAG):
-                    candidate_product(step - CANDIDATE_LAG)
-                for half in blends:
-                    blend_sum(half)
-                if exists(step - ADD_LAG):
-                    add_gh(step - ADD_LAG, 1)
-                if exists(step - CANDIDATE_LAG):
-                    candidate_sum(step - CANDIDATE_LAG)
-                if exists(step - CANDIDATE_LAG):
                     blend_keep(step - CANDIDATE_LAG)
+                if exists(step - CANDIDATE_LAG):
+                    blend_new(step - CANDIDATE_LAG)
+                if step < HALVES and exists(step - ADD_LAG):
+                    for s in range(PAIR):
+                        add_gh(step - ADD_LAG, s)
                 for s in range(PAIR):
                     if exists(step + X_LEAD):
                         transpose_x(step + X_LEAD, s)
+                if step == 0:
+                    nc.vector.tensor_copy(out=b_n[:], in_=b_n_ps[:])
                 if exists(step):
-                    for number in range(4):
-                        project_rz(step, number)
+                    project_rz(step)
+                if exists(step):
                     project_n(step)

@@ -26,6 +26,7 @@ RZ_TILES = 2 * HIDDEN // P
 ROW_TILES = ROWS // P
 PAIR = 2
 HALF_ROWS = PAIR * P
+BOTH = slice(0, PAIR)
 ROUND_ROWS = 2 * HALF_ROWS
 ROUNDS = ROWS // ROUND_ROWS
 HALVES = 2 * ROUNDS
@@ -64,7 +65,7 @@ def tile_grucellstack_pa_t_kernel(tc, x, h0, gh0, w_words, w_scales, b_ih0, out)
 
         x_of, gh_of, h_of = {}, {}, {}
         grouped_of, codes_of, planes_of, git_of = {}, {}, {}, {}
-        pre_of, keep_of, new_of = {}, {}, {}
+        pre_of, keep_of, new_of, out_of, xt_of = {}, {}, {}, {}, {}
         rz_of, n_of, gi_n_of, diff_of, acc_of, gi_rz_of = {}, {}, {}, {}, {}, {}
 
         def load_x(half):
@@ -86,6 +87,8 @@ def tile_grucellstack_pa_t_kernel(tc, x, h0, gh0, w_words, w_scales, b_ih0, out)
                 gh_of[first + i] = gh_sb[:, i * PAIR : (i + 1) * PAIR, :]
                 h_of[first + i] = h_sb[:, i * PAIR : (i + 1) * PAIR, :]
 
+        idle = const.tile([P, 512], BF16)
+        nc.vector.memset(idle[:], 0.0)
         warm = const.tile([P, 1], F32)
         nc.vector.memset(warm[:], 0.0)
         nc.scalar.activation(out=warm[:], in_=warm[:], func=ACT.Sigmoid)
@@ -100,6 +103,7 @@ def tile_grucellstack_pa_t_kernel(tc, x, h0, gh0, w_words, w_scales, b_ih0, out)
         nc.vector.memset(ones[:], 1.0)
 
         load_x(0)
+        load_x(1)
 
         w_codes = const.tile([P, PASSES, 2 * GATES], U8, align_bytes=64)
         nc.sync.dma_start(
@@ -113,7 +117,6 @@ def tile_grucellstack_pa_t_kernel(tc, x, h0, gh0, w_words, w_scales, b_ih0, out)
                 in_=w_scales[:, 4 * quad : 4 * quad + 4, :].rearrange("g r n -> r g n").bitcast(I32),
             )
 
-        load_x(1)
         load_gh_h(0, 1)
         load_x(2)
         load_gh_h(1, 1)
@@ -128,17 +131,20 @@ def tile_grucellstack_pa_t_kernel(tc, x, h0, gh0, w_words, w_scales, b_ih0, out)
         def transpose_x(half, s):
             if s == 0:
                 grouped_of[half] = quant.tile([P, PASSES, HALF_ROWS, PACK], BF16, align_bytes=64, name="grouped")
-            grouped_words = grouped_of[half][:].bitcast(F32)
             x_words = x_of[half][:, s, :].bitcast(F32)
             xt = psum.tile([P, PASSES, 2, P], F32, tag="bank")
             for g in range(PASSES):
                 for u in range(2):
                     words = slice(g * PASS_WORDS + u, (g + 1) * PASS_WORDS, 2)
                     nc.tensor.transpose(xt[:, g, u, :], x_words[:, words], ident[:])
+            xt_of[half, s] = xt
+
+        def copy_x(half, s):
+            grouped_words = grouped_of[half][:].bitcast(F32)
             copy_out = nc.vector.tensor_copy if half < X_HEAD and s == 1 else nc.scalar.copy
             copy_out(
                 out=grouped_words[:, :, s * P : (s + 1) * P, :],
-                in_=xt[:].rearrange("p g u r -> p g r u"),
+                in_=xt_of[half, s][:].rearrange("p g u r -> p g r u"),
             )
 
         def quantise(half):
@@ -220,18 +226,23 @@ def tile_grucellstack_pa_t_kernel(tc, x, h0, gh0, w_words, w_scales, b_ih0, out)
                 )
             nc.scalar.activation(out=rz_of[half][:, s, :], in_=gi_rz[:], func=ACT.Sigmoid)
 
-        def candidate_product(half):
-            n_gate = work.tile([P, PAIR, HIDDEN], F32)
+        def candidate_product(half, tiles=BOTH):
+            if half not in n_of:
+                n_of[half] = work.tile([P, PAIR, HIDDEN], F32, name="n_gate")
             nc.vector.tensor_tensor(
-                out=n_gate[:], in0=rz_of[half][:, :, 0:HIDDEN], in1=gh_of[half][:, :, 2 * HIDDEN : GATES], op=ALU.mult
+                out=n_of[half][:, tiles, :],
+                in0=rz_of[half][:, tiles, 0:HIDDEN],
+                in1=gh_of[half][:, tiles, 2 * HIDDEN : GATES],
+                op=ALU.mult,
             )
-            n_of[half] = n_gate
 
-        def candidate_sum(half):
-            nc.vector.tensor_tensor(out=n_of[half][:], in0=pre_of[half][:], in1=n_of[half][:], op=ALU.add)
+        def candidate_sum(half, tiles=BOTH):
+            n_gate = n_of[half][:, tiles, :]
+            nc.vector.tensor_tensor(out=n_gate, in0=pre_of[half][:, tiles, :], in1=n_gate, op=ALU.add)
 
-        def tanh_n(half):
-            nc.scalar.activation(out=n_of[half][:], in_=n_of[half][:], func=ACT.Tanh)
+        def tanh_n(half, tiles=BOTH):
+            n_gate = n_of[half][:, tiles, :]
+            nc.scalar.activation(out=n_gate, in_=n_gate, func=ACT.Tanh)
 
         def blend_keep(half):
             keep = work.tile([P, PAIR, HIDDEN], F32)
@@ -240,38 +251,53 @@ def tile_grucellstack_pa_t_kernel(tc, x, h0, gh0, w_words, w_scales, b_ih0, out)
             )
             keep_of[half] = keep
 
-        def blend_new(half):
-            n_gate = n_of[half]
-            new = work.tile([P, PAIR, HIDDEN], F32)
+        def blend_new(half, tiles=BOTH):
+            if half not in new_of:
+                new_of[half] = work.tile([P, PAIR, HIDDEN], F32, name="new")
             nc.vector.scalar_tensor_tensor(
-                out=new[:], in0=rz_of[half][:, :, HIDDEN : 2 * HIDDEN], scalar=1.0, in1=n_gate[:],
-                op0=ALU.subtract, op1=ALU.mult,
+                out=new_of[half][:, tiles, :],
+                in0=rz_of[half][:, tiles, HIDDEN : 2 * HIDDEN],
+                scalar=1.0,
+                in1=n_of[half][:, tiles, :],
+                op0=ALU.subtract,
+                op1=ALU.mult,
             )
-            new_of[half] = new
 
-        def blend_sum(half):
-            out_sb = work.tile([P, PAIR, HIDDEN], F32)
-            nc.vector.tensor_tensor(out=out_sb[:], in0=keep_of[half][:], in1=new_of[half][:], op=ALU.subtract)
-            nc.sync.dma_start(out=out_rows[:, half * PAIR : (half + 1) * PAIR, :], in_=out_sb[:])
+        def blend_sum(half, tiles=BOTH):
+            if half not in out_of:
+                out_of[half] = work.tile([P, PAIR, HIDDEN], F32, name="out_sb")
+            out_sb = out_of[half][:, tiles, :]
+            nc.vector.tensor_tensor(
+                out=out_sb, in0=keep_of[half][:, tiles, :], in1=new_of[half][:, tiles, :], op=ALU.subtract
+            )
+            nc.sync.dma_start(out=out_rows[:, half * PAIR + tiles.start : half * PAIR + tiles.stop, :], in_=out_sb)
 
         def exists(half):
             return 0 <= half < HALVES
 
         with tc.manual_schedule(engines={mybir.EngineType.PE, mybir.EngineType.Activation, mybir.EngineType.DVE}):
+            idle_ps = psum.tile([P, 512], F32, tag="bank")
+            for number in range(3):
+                nc.tensor.matmul(idle_ps[:], lhsT=idle[:, 0:P], rhs=idle[:], start=True, stop=True)
             bias_rows_f32 = const.tile([P, P], F32)
-            nc.vector.tensor_copy(out=bias_rows_f32[:], in_=bias_rows[:])
+            bias_col = const.tile([P, GATE_TILES], F32)
+            b_n = const.tile([P, PAIR, HIDDEN], F32)
             for s in range(PAIR):
                 transpose_x(0, s)
+                copy_x(0, s)
+            for s in range(PAIR):
+                transpose_x(1, s)
+            quantise(0)
+            nc.vector.tensor_copy(out=bias_rows_f32[:], in_=bias_rows[:])
+            for s in range(PAIR):
+                copy_x(1, s)
             bias_ps = psum.tile([P, PAIR, HIDDEN], F32, tag="bank")
             nc.tensor.transpose(bias_ps[:, 0, 0:P], bias_rows_f32[:], ident[:])
-            quantise(0)
-            bias_col = const.tile([P, GATE_TILES], F32)
             nc.vector.tensor_copy(out=bias_col[:], in_=bias_ps[:, 0, 0:GATE_TILES])
             b_n_ps = psum.tile([P, PAIR, HIDDEN], F32, tag="bank")
             for s in range(PAIR):
                 nc.tensor.matmul(b_n_ps[:, s, :], lhsT=ones[:], rhs=bn_row[:], start=True, stop=True)
-            b_n = const.tile([P, PAIR, HIDDEN], F32)
-            for step in range(LAST_STEP + 1):
+            for step in range(HALVES + 1):
                 if exists(step + X_LEAD + X_LOAD_LEAD):
                     load_x(step + X_LEAD + X_LOAD_LEAD)
                 first_use = step + GH_LOAD_LEAD
@@ -280,9 +306,6 @@ def tile_grucellstack_pa_t_kernel(tc, x, h0, gh0, w_words, w_scales, b_ih0, out)
                 for s in range(PAIR):
                     if exists(step - ADD_LAG):
                         open_rz(step - ADD_LAG, s)
-                if step >= HALVES and exists(step - ADD_LAG):
-                    for s in range(PAIR):
-                        add_gh(step - ADD_LAG, s)
                 if exists(step - CANDIDATE_LAG):
                     candidate_product(step - CANDIDATE_LAG)
                 if exists(step - BLEND_LAG):
@@ -299,15 +322,31 @@ def tile_grucellstack_pa_t_kernel(tc, x, h0, gh0, w_words, w_scales, b_ih0, out)
                     blend_keep(step - CANDIDATE_LAG)
                 if exists(step - CANDIDATE_LAG):
                     blend_new(step - CANDIDATE_LAG)
-                if step < HALVES and exists(step - ADD_LAG):
-                    for s in range(PAIR):
+                for s in range(PAIR):
+                    if exists(step - ADD_LAG):
                         add_gh(step - ADD_LAG, s)
                 for s in range(PAIR):
-                    if exists(step + X_LEAD):
+                    if step > 0 and exists(step + X_LEAD):
                         transpose_x(step + X_LEAD, s)
+                for s in range(PAIR):
+                    if step > 0 and exists(step + X_LEAD):
+                        copy_x(step + X_LEAD, s)
                 if step == 0:
                     nc.vector.tensor_copy(out=b_n[:], in_=b_n_ps[:])
                 if exists(step):
                     project_rz(step)
                 if exists(step):
                     project_n(step)
+            last = HALVES - 1
+            candidate_product(last, slice(0, 1))
+            blend_sum(last - 1)
+            candidate_product(last, slice(1, 2))
+            blend_keep(last)
+            for s in range(PAIR):
+                candidate_sum(last, slice(s, s + 1))
+            for s in range(PAIR):
+                tanh_n(last, slice(s, s + 1))
+            for s in range(PAIR):
+                blend_new(last, slice(s, s + 1))
+            for s in range(PAIR):
+                blend_sum(last, slice(s, s + 1))

@@ -287,8 +287,8 @@ def tile_grucellstack_pa_t_kernel(tc, x, h0, gh0, w_words, w_scales, b_ih0, out)
                 copy_x(0, s)
             for s in range(PAIR):
                 transpose_x(1, s)
-            quantise(0)
             nc.vector.tensor_copy(out=bias_rows_f32[:], in_=bias_rows[:])
+            quantise(0)
             for s in range(PAIR):
                 copy_x(1, s)
             bias_ps = psum.tile([P, PAIR, HIDDEN], F32, tag="bank")
@@ -306,31 +306,31 @@ def tile_grucellstack_pa_t_kernel(tc, x, h0, gh0, w_words, w_scales, b_ih0, out)
                 for s in range(PAIR):
                     if exists(step - ADD_LAG):
                         open_rz(step - ADD_LAG, s)
-                if exists(step - CANDIDATE_LAG):
-                    candidate_product(step - CANDIDATE_LAG)
-                if exists(step - BLEND_LAG):
-                    blend_sum(step - BLEND_LAG)
-                if exists(step - CANDIDATE_LAG):
-                    candidate_sum(step - CANDIDATE_LAG)
                 if step > 0 and exists(step):
                     quantise(step)
                 if exists(step - CANDIDATE_LAG):
-                    tanh_n(step - CANDIDATE_LAG)
+                    candidate_product(step - CANDIDATE_LAG)
+                if exists(step - BLEND_LAG):
+                    blend_new(step - BLEND_LAG)
+                if exists(step - CANDIDATE_LAG):
+                    candidate_sum(step - CANDIDATE_LAG)
+                if exists(step - BLEND_LAG):
+                    blend_sum(step - BLEND_LAG)
                 if exists(step - PRE_LAG):
                     bias_n(step - PRE_LAG)
                 if exists(step - CANDIDATE_LAG):
                     blend_keep(step - CANDIDATE_LAG)
-                if exists(step - CANDIDATE_LAG):
-                    blend_new(step - CANDIDATE_LAG)
-                for s in range(PAIR):
-                    if exists(step - ADD_LAG):
-                        add_gh(step - ADD_LAG, s)
                 for s in range(PAIR):
                     if step > 0 and exists(step + X_LEAD):
                         transpose_x(step + X_LEAD, s)
                 for s in range(PAIR):
                     if step > 0 and exists(step + X_LEAD):
                         copy_x(step + X_LEAD, s)
+                for s in range(PAIR):
+                    if exists(step - ADD_LAG):
+                        add_gh(step - ADD_LAG, s)
+                if exists(step - CANDIDATE_LAG):
+                    tanh_n(step - CANDIDATE_LAG)
                 if step == 0:
                     nc.vector.tensor_copy(out=b_n[:], in_=b_n_ps[:])
                 if exists(step):
@@ -339,11 +339,12 @@ def tile_grucellstack_pa_t_kernel(tc, x, h0, gh0, w_words, w_scales, b_ih0, out)
                     project_n(step)
             last = HALVES - 1
             candidate_product(last, slice(0, 1))
-            blend_sum(last - 1)
+            blend_new(last - 1)
             candidate_product(last, slice(1, 2))
             blend_keep(last)
             for s in range(PAIR):
                 candidate_sum(last, slice(s, s + 1))
+            blend_sum(last - 1)
             for s in range(PAIR):
                 tanh_n(last, slice(s, s + 1))
             for s in range(PAIR):

@@ -70,7 +70,7 @@ def tile_grucellstack_pa_t_kernel(tc, x, h0, gh0, w_words, w_scales, b_ih0, out)
 
         def load_x(half):
             x_sb = x_pool.tile([P, PAIR, K], BF16)
-            if half < 2:
+            if half == 0:
                 for s in range(PAIR):
                     nc.sync.dma_start(out=x_sb[:, s, :], in_=x_rows[:, half * PAIR + s, :])
             else:
@@ -87,6 +87,8 @@ def tile_grucellstack_pa_t_kernel(tc, x, h0, gh0, w_words, w_scales, b_ih0, out)
                 gh_of[first + i] = gh_sb[:, i * PAIR : (i + 1) * PAIR, :]
                 h_of[first + i] = h_sb[:, i * PAIR : (i + 1) * PAIR, :]
 
+        w_planes = const.tile([P, PASSES, GATES], U8, align_bytes=64)
+        nc.vector.memset(w_planes[:].bitcast(I32), 0)
         idle = const.tile([P, 512], BF16)
         nc.vector.memset(idle[:], 0.0)
         warm = const.tile([P, 1], F32)
@@ -105,18 +107,16 @@ def tile_grucellstack_pa_t_kernel(tc, x, h0, gh0, w_words, w_scales, b_ih0, out)
         load_x(0)
         load_x(1)
 
-        w_codes = const.tile([P, PASSES, 2 * GATES], U8, align_bytes=64)
-        nc.sync.dma_start(
-            out=w_codes[:].bitcast(I32), in_=w_words.rearrange("g p b -> p g b").bitcast(I32)
-        )
-        w_planes = const.tile([P, PASSES, GATES], U8, align_bytes=64)
-        nc.vector.memset(w_planes[:].bitcast(I32), 0)
         for quad in range(4):
             nc.sync.dma_start(
                 out=w_planes[32 * quad : 32 * quad + 4].bitcast(I32),
                 in_=w_scales[:, 4 * quad : 4 * quad + 4, :].rearrange("g r n -> r g n").bitcast(I32),
             )
 
+        w_codes = const.tile([P, PASSES, 2 * GATES], U8, align_bytes=64)
+        nc.sync.dma_start(
+            out=w_codes[:].bitcast(I32), in_=w_words.rearrange("g p b -> p g b").bitcast(I32)
+        )
         load_gh_h(0, 1)
         load_x(2)
         load_gh_h(1, 1)
@@ -156,31 +156,38 @@ def tile_grucellstack_pa_t_kernel(tc, x, h0, gh0, w_words, w_scales, b_ih0, out)
                 in_=grouped_of[half][:].rearrange("p g r t -> p (g r t)"),
             )
 
+        def project_columns(half, first):
+            if half not in git_of:
+                git_of[half] = git_pool.tile([P, GATE_TILES, HALF_ROWS], F32, name="gi_t")
+            acc = psum.tile([P, 2, HALF_ROWS], F32, tag="bank")
+            for i in range(2):
+                j = first + i
+                for s in range(PAIR):
+                    rows = slice(s * P, (s + 1) * P)
+                    for g in range(PASSES):
+                        nc.tensor.matmul_mx(
+                            out=acc[:, i, rows],
+                            lhsT=w_codes[:, g, 2 * P * j : 2 * P * (j + 1)].bitcast(FP4X4),
+                            lhsT_scale=w_planes[:, g, P * j : P * (j + 1)],
+                            rhs=codes_of[half][:, g, rows].bitcast(FP8X4),
+                            rhs_scale=planes_of[half][:, g, rows],
+                            start=(g == 0),
+                            stop=(g == PASSES - 1),
+                        )
+            for i in range(2):
+                j = first + i
+                nc.scalar.activation(
+                    out=git_of[half][:, j, :], in_=acc[:, i, :], func=ACT.Identity, bias=bias_col[:, j : j + 1]
+                )
+
         def project_rz(half):
-            git_of[half] = git_pool.tile([P, RZ_TILES, HALF_ROWS], F32, name="gi_t")
             for first in range(0, RZ_TILES, 2):
-                acc = psum.tile([P, 2, HALF_ROWS], F32, tag="bank")
-                for i in range(2):
-                    j = first + i
-                    for s in range(PAIR):
-                        rows = slice(s * P, (s + 1) * P)
-                        for g in range(PASSES):
-                            nc.tensor.matmul_mx(
-                                out=acc[:, i, rows],
-                                lhsT=w_codes[:, g, 2 * P * j : 2 * P * (j + 1)].bitcast(FP4X4),
-                                lhsT_scale=w_planes[:, g, P * j : P * (j + 1)],
-                                rhs=codes_of[half][:, g, rows].bitcast(FP8X4),
-                                rhs_scale=planes_of[half][:, g, rows],
-                                start=(g == 0),
-                                stop=(g == PASSES - 1),
-                            )
-                for i in range(2):
-                    j = first + i
-                    nc.scalar.activation(
-                        out=git_of[half][:, j, :], in_=acc[:, i, :], func=ACT.Identity, bias=bias_col[:, j : j + 1]
-                    )
+                project_columns(half, first)
 
         def project_n(half):
+            if biased(half):
+                project_columns(half, RZ_TILES)
+                return
             gi_n = psum.tile([P, PAIR, HIDDEN], F32, tag="bank")
             for s in range(PAIR):
                 rows = slice(s * P, (s + 1) * P)
@@ -197,6 +204,17 @@ def tile_grucellstack_pa_t_kernel(tc, x, h0, gh0, w_words, w_scales, b_ih0, out)
                             stop=(g == PASSES - 1),
                         )
             gi_n_of[half] = gi_n
+
+        def transpose_n(half):
+            pre_n = psum.tile([P, PAIR, HIDDEN], F32, tag="bank")
+            for s in range(PAIR):
+                for c in range(HIDDEN // P):
+                    nc.tensor.transpose(
+                        pre_n[:, s, c * P : (c + 1) * P],
+                        git_of[half][:, RZ_TILES + c, s * P : (s + 1) * P],
+                        ident[:],
+                    )
+            pre_of[half] = pre_n
 
         def bias_n(half):
             pre_n = work.tile([P, PAIR, HIDDEN], F32)
@@ -272,6 +290,9 @@ def tile_grucellstack_pa_t_kernel(tc, x, h0, gh0, w_words, w_scales, b_ih0, out)
             )
             nc.sync.dma_start(out=out_rows[:, half * PAIR + tiles.start : half * PAIR + tiles.stop, :], in_=out_sb)
 
+        def biased(half):
+            return half == HALVES - 1
+
         def exists(half):
             return 0 <= half < HALVES
 
@@ -316,7 +337,7 @@ def tile_grucellstack_pa_t_kernel(tc, x, h0, gh0, w_words, w_scales, b_ih0, out)
                     candidate_sum(step - CANDIDATE_LAG)
                 if exists(step - BLEND_LAG):
                     blend_sum(step - BLEND_LAG)
-                if exists(step - PRE_LAG):
+                if exists(step - PRE_LAG) and not biased(step - PRE_LAG):
                     bias_n(step - PRE_LAG)
                 if exists(step - CANDIDATE_LAG):
                     blend_keep(step - CANDIDATE_LAG)
@@ -329,6 +350,8 @@ def tile_grucellstack_pa_t_kernel(tc, x, h0, gh0, w_words, w_scales, b_ih0, out)
                 for s in range(PAIR):
                     if exists(step - ADD_LAG):
                         add_gh(step - ADD_LAG, s)
+                if exists(step - ADD_LAG) and biased(step - ADD_LAG):
+                    transpose_n(step - ADD_LAG)
                 if exists(step - CANDIDATE_LAG):
                     tanh_n(step - CANDIDATE_LAG)
                 if step == 0:
@@ -339,9 +362,9 @@ def tile_grucellstack_pa_t_kernel(tc, x, h0, gh0, w_words, w_scales, b_ih0, out)
                     project_n(step)
             last = HALVES - 1
             candidate_product(last, slice(0, 1))
-            blend_new(last - 1)
             candidate_product(last, slice(1, 2))
             blend_keep(last)
+            blend_new(last - 1)
             for s in range(PAIR):
                 candidate_sum(last, slice(s, s + 1))
             blend_sum(last - 1)

@@ -87,10 +87,8 @@ def tile_grucellstack_pa_t_kernel(tc, x, h0, gh0, w_words, w_scales, b_ih0, out)
                 gh_of[first + i] = gh_sb[:, i * PAIR : (i + 1) * PAIR, :]
                 h_of[first + i] = h_sb[:, i * PAIR : (i + 1) * PAIR, :]
 
-        w_planes = const.tile([P, PASSES, GATES], U8, align_bytes=64)
-        nc.vector.memset(w_planes[:].bitcast(I32), 0)
         idle = const.tile([P, 512], BF16)
-        nc.vector.memset(idle[:], 0.0)
+        nc.gpsimd.memset(idle[:].bitcast(F32), 0.0)
         warm = const.tile([P, 1], F32)
         nc.vector.memset(warm[:], 0.0)
         nc.scalar.activation(out=warm[:], in_=warm[:], func=ACT.Sigmoid)
@@ -103,6 +101,9 @@ def tile_grucellstack_pa_t_kernel(tc, x, h0, gh0, w_words, w_scales, b_ih0, out)
         nc.scalar.dma_start(out=bn_row[0:1, :], in_=b_ih0[2 * HIDDEN : GATES].rearrange("(o c) -> o c", o=1))
         ones = const.tile([P, P], BF16)
         nc.vector.memset(ones[:], 1.0)
+
+        w_planes = const.tile([P, PASSES, GATES], U8, align_bytes=64)
+        nc.vector.memset(w_planes[:].bitcast(I32), 0)
 
         load_x(0)
         load_x(1)
@@ -298,7 +299,7 @@ def tile_grucellstack_pa_t_kernel(tc, x, h0, gh0, w_words, w_scales, b_ih0, out)
 
         with tc.manual_schedule(engines={mybir.EngineType.PE, mybir.EngineType.Activation, mybir.EngineType.DVE}):
             idle_ps = psum.tile([P, 512], F32, tag="bank")
-            for number in range(3):
+            for number in range(4):
                 nc.tensor.matmul(idle_ps[:], lhsT=idle[:, 0:P], rhs=idle[:], start=True, stop=True)
             bias_rows_f32 = const.tile([P, P], F32)
             bias_col = const.tile([P, GATE_TILES], F32)
@@ -324,9 +325,6 @@ def tile_grucellstack_pa_t_kernel(tc, x, h0, gh0, w_words, w_scales, b_ih0, out)
                 first_use = step + GH_LOAD_LEAD
                 if exists(first_use) and first_use % 2 == 0:
                     load_gh_h(first_use, 2)
-                for s in range(PAIR):
-                    if exists(step - ADD_LAG):
-                        open_rz(step - ADD_LAG, s)
                 if step > 0 and exists(step):
                     quantise(step)
                 if exists(step - CANDIDATE_LAG):
@@ -347,6 +345,9 @@ def tile_grucellstack_pa_t_kernel(tc, x, h0, gh0, w_words, w_scales, b_ih0, out)
                 for s in range(PAIR):
                     if step > 0 and exists(step + X_LEAD):
                         copy_x(step + X_LEAD, s)
+                for s in range(PAIR):
+                    if exists(step - ADD_LAG):
+                        open_rz(step - ADD_LAG, s)
                 for s in range(PAIR):
                     if exists(step - ADD_LAG):
                         add_gh(step - ADD_LAG, s)

@@ -118,8 +118,8 @@ def tile_grucellstack_pa_t_kernel(tc, x, h0, gh0, w_words, w_scales, b_ih0, out)
         nc.sync.dma_start(
             out=w_codes[:].bitcast(I32), in_=w_words.rearrange("g p b -> p g b").bitcast(I32)
         )
-        load_gh_h(0, 1)
         load_x(2)
+        load_gh_h(0, 1)
         load_gh_h(1, 1)
         for half in range(3, X_LEAD + X_LOAD_LEAD):
             load_x(half)

@@ -33,7 +33,7 @@ HALVES = 2 * ROUNDS
 
 X_LEAD = 1
 ADD_LAG = 1
-PRE_LAG = 1
+PRE_LAG = 2
 X_HEAD = 3
 CANDIDATE_LAG = 2
 TANH_LAG = 4
@@ -96,11 +96,6 @@ def tile_grucellstack_pa_t_kernel(tc, x, h0, gh0, w_words, w_scales, b_ih0, out)
         bias_rows = const.tile([P, P], BF16)
         nc.vector.memset(bias_rows[:], 0.0)
         nc.scalar.dma_start(out=bias_rows[0:GATE_TILES, :], in_=b_ih0.rearrange("(j c) -> j c", c=P))
-        bn_row = const.tile([P, HIDDEN], BF16)
-        nc.vector.memset(bn_row[:], 0.0)
-        nc.scalar.dma_start(out=bn_row[0:1, :], in_=b_ih0[2 * HIDDEN : GATES].rearrange("(o c) -> o c", o=1))
-        ones = const.tile([P, P], BF16)
-        nc.vector.memset(ones[:], 1.0)
 
         w_planes = const.tile([P, PASSES, GATES], U8, align_bytes=64)
         nc.vector.memset(w_planes[:].bitcast(I32), 0)
@@ -318,7 +313,15 @@ def tile_grucellstack_pa_t_kernel(tc, x, h0, gh0, w_words, w_scales, b_ih0, out)
             nc.vector.tensor_copy(out=bias_col[:], in_=bias_ps[:, 0, 0:GATE_TILES])
             b_n_ps = psum.tile([P, PAIR, HIDDEN], F32, tag="bank")
             for s in range(PAIR):
-                nc.tensor.matmul(b_n_ps[:, s, :], lhsT=ones[:], rhs=bn_row[:], start=True, stop=True)
+                for c in range(HIDDEN // P):
+                    row = RZ_TILES + c
+                    nc.tensor.matmul(
+                        b_n_ps[:, s, c * P : (c + 1) * P],
+                        lhsT=ident_bf16[:, row : row + 1].to_broadcast([P, P]),
+                        rhs=bias_rows[:],
+                        start=True,
+                        stop=True,
+                    )
             for step in range(HALVES + 1):
                 if exists(step + X_LEAD + X_LOAD_LEAD):
                     load_x(step + X_LEAD + X_LOAD_LEAD)
@@ -327,6 +330,8 @@ def tile_grucellstack_pa_t_kernel(tc, x, h0, gh0, w_words, w_scales, b_ih0, out)
                     load_gh_h(first_use, 2)
                 if step > 0 and exists(step):
                     quantise(step)
+                if exists(step - PRE_LAG) and not biased(step - PRE_LAG):
+                    bias_n(step - PRE_LAG)
                 if exists(step - CANDIDATE_LAG):
                     candidate_product(step - CANDIDATE_LAG)
                 if exists(step - BLEND_LAG):
@@ -335,8 +340,6 @@ def tile_grucellstack_pa_t_kernel(tc, x, h0, gh0, w_words, w_scales, b_ih0, out)
                     candidate_sum(step - CANDIDATE_LAG)
                 if exists(step - BLEND_LAG):
                     blend_sum(step - BLEND_LAG)
-                if exists(step - PRE_LAG) and not biased(step - PRE_LAG):
-                    bias_n(step - PRE_LAG)
                 if exists(step - CANDIDATE_LAG):
                     blend_keep(step - CANDIDATE_LAG)
                 for s in range(PAIR):
@@ -357,9 +360,11 @@ def tile_grucellstack_pa_t_kernel(tc, x, h0, gh0, w_words, w_scales, b_ih0, out)
                     tanh_n(step - CANDIDATE_LAG)
                 if step == 0:
                     nc.vector.tensor_copy(out=b_n[:], in_=b_n_ps[:])
+                if exists(step - 1) and step < HALVES:
+                    project_n(step - 1)
                 if exists(step):
                     project_rz(step)
-                if exists(step):
+                if step == HALVES - 1:
                     project_n(step)
             last = HALVES - 1
             candidate_product(last, slice(0, 1))

from contextlib import ExitStack

import concourse.mybir as mybir
from concourse.masks import make_identity

F32 = mybir.dt.float32
BF16 = mybir.dt.bfloat16
I32 = mybir.dt.int32
U32 = mybir.dt.uint32
U8 = mybir.dt.uint8
FP8X4 = mybir.dt.float8_e4m3fn_x4
FP4X4 = mybir.dt.float4_e2m1fn_x4
ACT = mybir.ActivationFunctionType
ALU = mybir.AluOpType

P = 128
PACK = 4
K_PASS = P * PACK

ROWS, K, HIDDEN = 4096, 1024, 256
GATES = 3 * HIDDEN
PASSES = K // K_PASS
PASS_WORDS = K_PASS // 2
GATE_TILES = GATES // P
RZ_TILES = 2 * HIDDEN // P
ROW_TILES = ROWS // P
PAIR = 2
HALF_ROWS = PAIR * P
BOTH = slice(0, PAIR)
ROUND_ROWS = 2 * HALF_ROWS
ROUNDS = ROWS // ROUND_ROWS
HALVES = 2 * ROUNDS

X_LEAD = 1
ADD_LAG = 1
PRE_LAG = 2
X_HEAD = 3
CANDIDATE_LAG = 2
TANH_LAG = 4
BLEND_LAG = 3
X_LOAD_LEAD = 5
GH_LOAD_LEAD = 2

LAST_STEP = HALVES + BLEND_LAG - 1

FLOPS = 2 * ROWS * K * GATES


def tile_grucellstack_pa_t_kernel(tc, x, h0, gh0, w_words, w_scales, b_ih0, out):
    nc = tc.nc

    x_rows = x.rearrange("(p t) k -> p t k", t=ROW_TILES)
    gh_rows = gh0.rearrange("(p t) c -> p t c", t=ROW_TILES)
    h_rows = h0.rearrange("(p t) c -> p t c", t=ROW_TILES)
    out_rows = out.rearrange("(p t) c -> p t c", t=ROW_TILES)

    with ExitStack() as ctx:
        const = ctx.enter_context(tc.tile_pool(name="const", bufs=1))
        x_pool = ctx.enter_context(tc.tile_pool(name="x_pool", bufs=X_LEAD + X_LOAD_LEAD + 1))
        gh_pool = ctx.enter_context(tc.tile_pool(name="gh_pool", bufs=(GH_LOAD_LEAD + BLEND_LAG) // 2 + 1))
        quant = ctx.enter_context(tc.tile_pool(name="quant", bufs=4))
        git_pool = ctx.enter_context(tc.tile_pool(name="git_pool", bufs=4))
        work = ctx.enter_context(tc.tile_pool(name="work", bufs=4))
        psum = ctx.enter_context(tc.psum_pool(name="psum", bufs=8))

        x_of, gh_of, h_of = {}, {}, {}
        grouped_of, codes_of, planes_of, git_of = {}, {}, {}, {}
        pre_of, keep_of, new_of, out_of, xt_of = {}, {}, {}, {}, {}
        rz_of, n_of, gi_n_of, diff_of, acc_of, gi_rz_of = {}, {}, {}, {}, {}, {}

        def load_x(half):
            x_sb = x_pool.tile([P, PAIR, K], BF16)
            if half == 0:
                for s in range(PAIR):
                    nc.sync.dma_start(out=x_sb[:, s, :], in_=x_rows[:, half * PAIR + s, :])
            else:
                nc.sync.dma_start(out=x_sb[:], in_=x_rows[:, half * PAIR : (half + 1) * PAIR, :])
            x_of[half] = x_sb

        def load_gh_h(first, count):
            tiles = slice(first * PAIR, (first + count) * PAIR)
            gh_sb = gh_pool.tile([P, 2 * PAIR, GATES], BF16)
            nc.sync.dma_start(out=gh_sb[:, 0 : count * PAIR, :], in_=gh_rows[:, tiles, :])
            h_sb = gh_pool.tile([P, 2 * PAIR, HIDDEN], BF16)
            nc.sync.dma_start(out=h_sb[:, 0 : count * PAIR, :], in_=h_rows[:, tiles, :])
            for i in range(count):
                gh_of[first + i] = gh_sb[:, i * PAIR : (i + 1) * PAIR, :]
                h_of[first + i] = h_sb[:, i * PAIR : (i + 1) * PAIR, :]

        idle = const.tile([P, 512], BF16)
        nc.gpsimd.memset(idle[:].bitcast(F32), 0.0)
        warm = const.tile([P, 1], F32)
        nc.vector.memset(warm[:], 0.0)
        nc.scalar.activation(out=warm[:], in_=warm[:], func=ACT.Sigmoid)

        bias_rows = const.tile([P, P], BF16)
        nc.vector.memset(bias_rows[:], 0.0)
        nc.scalar.dma_start(out=bias_rows[0:GATE_TILES, :], in_=b_ih0.rearrange("(j c) -> j c", c=P))

        w_planes = const.tile([P, PASSES, GATES], U8, align_bytes=64)
        nc.vector.memset(w_planes[:].bitcast(I32), 0)

        load_x(0)
        load_x(1)

        for quad in range(4):
            nc.sync.dma_start(
                out=w_planes[32 * quad : 32 * quad + 4].bitcast(I32),
                in_=w_scales[:, 4 * quad : 4 * quad + 4, :].rearrange("g r n -> r g n").bitcast(I32),
            )

        w_codes = const.tile([P, PASSES, 2 * GATES], U8, align_bytes=64)
        nc.sync.dma_start(
            out=w_codes[:].bitcast(I32), in_=w_words.rearrange("g p b -> p g b").bitcast(I32)
        )
        load_x(2)
        load_gh_h(0, 1)
        load_gh_h(1, 1)
        for half in range(3, X_LEAD + X_LOAD_LEAD):
            load_x(half)

        ident = const.tile([P, P], F32)
        make_identity(nc, ident[:])
        ident_bf16 = const.tile([P, P], BF16)
        make_identity(nc, ident_bf16[:])

        def transpose_x(half, s):
            if s == 0:
                grouped_of[half] = quant.tile([P, PASSES, HALF_ROWS, PACK], BF16, align_bytes=64, name="grouped")
            x_words = x_of[half][:, s, :].bitcast(F32)
            xt = psum.tile([P, PASSES, 2, P], F32, tag="bank")
            for g in range(PASSES):
                for u in range(2):
                    words = slice(g * PASS_WORDS + u, (g + 1) * PASS_WORDS, 2)
                    nc.tensor.transpose(xt[:, g, u, :], x_words[:, words], ident[:])
            xt_of[half, s] = xt

        def copy_x(half, s):
            grouped_words = grouped_of[half][:].bitcast(F32)
            copy_out = nc.vector.tensor_copy if half < X_HEAD and s == 1 else nc.scalar.copy
            copy_out(
                out=grouped_words[:, :, s * P : (s + 1) * P, :],
                in_=xt_of[half, s][:].rearrange("p g u r -> p g r u"),
            )

        def quantise(half):
            codes_of[half] = quant.tile([P, PASSES, HALF_ROWS], U32, align_bytes=64, name="x_codes")
            planes_of[half] = quant.tile([P, PASSES, HALF_ROWS], U8, align_bytes=64, name="x_planes")
            nc.vector.quantize_mx(
                out=codes_of[half][:].rearrange("p g r -> p (g r)").bitcast(FP8X4),
                scales=planes_of[half][:].rearrange("p g r -> p (g r)"),
                in_=grouped_of[half][:].rearrange("p g r t -> p (g r t)"),
            )

        def project_columns(half, first):
            if half not in git_of:
                git_of[half] = git_pool.tile([P, GATE_TILES, HALF_ROWS], F32, name="gi_t")
            acc = psum.tile([P, 2, HALF_ROWS], F32, tag="bank")
            for i in range(2):
                j = first + i
                for s in range(PAIR):
                    rows = slice(s * P, (s + 1) * P)
                    for g in range(PASSES):
                        nc.tensor.matmul_mx(
                            out=acc[:, i, rows],
                            lhsT=w_codes[:, g, 2 * P * j : 2 * P * (j + 1)].bitcast(FP4X4),
                            lhsT_scale=w_planes[:, g, P * j : P * (j + 1)],
                            rhs=codes_of[half][:, g, rows].bitcast(FP8X4),
                            rhs_scale=planes_of[half][:, g, rows],
                            start=(g == 0),
                            stop=(g == PASSES - 1),
                        )
            for i in range(2):
                j = first + i
                nc.scalar.activation(
                    out=git_of[half][:, j, :], in_=acc[:, i, :], func=ACT.Identity, bias=bias_col[:, j : j + 1]
                )

        def project_rz(half):
            for first in range(0, RZ_TILES, 2):
                project_columns(half, first)

        def project_n(half):
            if biased(half):
                project_columns(half, RZ_TILES)
                return
            gi_n = psum.tile([P, PAIR, HIDDEN], F32, tag="bank")
            for s in range(PAIR):
                rows = slice(s * P, (s + 1) * P)
                for c in range(HIDDEN // P):
                    j = RZ_TILES + c
                    for g in range(PASSES):
                        nc.tensor.matmul_mx(
                            out=gi_n[:, s, c * P : (c + 1) * P],
                            lhsT=codes_of[half][:, g, rows].bitcast(FP8X4),
                            lhsT_scale=planes_of[half][:, g, rows],
                            rhs=w_codes[:, g, 2 * P * j : 2 * P * (j + 1)].bitcast(FP4X4),
                            rhs_scale=w_planes[:, g, P * j : P * (j + 1)],
                            start=(g == 0),
                            stop=(g == PASSES - 1),
                        )
            gi_n_of[half] = gi_n

        def transpose_n(half):
            pre_n = psum.tile([P, PAIR, HIDDEN], F32, tag="bank")
            for s in range(PAIR):
                for c in range(HIDDEN // P):
                    nc.tensor.transpose(
                        pre_n[:, s, c * P : (c + 1) * P],
                        git_of[half][:, RZ_TILES + c, s * P : (s + 1) * P],
                        ident[:],
                    )
            pre_of[half] = pre_n

        def bias_n(half):
            pre_n = work.tile([P, PAIR, HIDDEN], F32)
            nc.vector.tensor_tensor(out=pre_n[:], in0=gi_n_of[half][:], in1=b_n[:], op=ALU.add)
            pre_of[half] = pre_n

        def open_rz(half, s):
            gi_rz = psum.tile([P, 2 * HIDDEN], F32, tag="bank")
            nc.tensor.matmul(
                gi_rz[:], lhsT=ident_bf16[:], rhs=gh_of[half][:, s, 0 : 2 * HIDDEN], start=True, stop=False
            )
            gi_rz_of[half, s] = gi_rz

        def add_gh(half, s):
            if s == 0:
                rz_of[half] = work.tile([P, PAIR, 2 * HIDDEN], F32, name="rz")
            rows = slice(s * P, (s + 1) * P)
            gi_rz = gi_rz_of[half, s]
            for j in range(RZ_TILES):
                nc.tensor.matmul(
                    gi_rz[:, j * P : (j + 1) * P],
                    lhsT=git_of[half][:, j, rows],
                    rhs=ident[:],
                    is_transpose=True,
                    start=False,
                    stop=(j == RZ_TILES - 1),
                )
            nc.scalar.activation(out=rz_of[half][:, s, :], in_=gi_rz[:], func=ACT.Sigmoid)

        def candidate_product(half, tiles=BOTH):
            if half not in n_of:
                n_of[half] = work.tile([P, PAIR, HIDDEN], F32, name="n_gate")
            nc.vector.tensor_tensor(
                out=n_of[half][:, tiles, :],
                in0=rz_of[half][:, tiles, 0:HIDDEN],
                in1=gh_of[half][:, tiles, 2 * HIDDEN : GATES],
                op=ALU.mult,
            )

        def candidate_sum(half, tiles=BOTH):
            n_gate = n_of[half][:, tiles, :]
            nc.vector.tensor_tensor(out=n_gate, in0=pre_of[half][:, tiles, :], in1=n_gate, op=ALU.add)

        def tanh_n(half, tiles=BOTH):
            n_gate = n_of[half][:, tiles, :]
            nc.scalar.activation(out=n_gate, in_=n_gate, func=ACT.Tanh)

        def blend_keep(half):
            keep = work.tile([P, PAIR, HIDDEN], F32)
            nc.vector.tensor_tensor(
                out=keep[:], in0=rz_of[half][:, :, HIDDEN : 2 * HIDDEN], in1=h_of[half], op=ALU.mult
            )
            keep_of[half] = keep

        def blend_new(half, tiles=BOTH):
            if half not in new_of:
                new_of[half] = work.tile([P, PAIR, HIDDEN], F32, name="new")
            nc.vector.scalar_tensor_tensor(
                out=new_of[half][:, tiles, :],
                in0=rz_of[half][:, tiles, HIDDEN : 2 * HIDDEN],
                scalar=1.0,
                in1=n_of[half][:, tiles, :],
                op0=ALU.subtract,
                op1=ALU.mult,
            )

        def blend_sum(half, tiles=BOTH):
            if half not in out_of:
                out_of[half] = work.tile([P, PAIR, HIDDEN], F32, name="out_sb")
            out_sb = out_of[half][:, tiles, :]
            nc.vector.tensor_tensor(
                out=out_sb, in0=keep_of[half][:, tiles, :], in1=new_of[half][:, tiles, :], op=ALU.subtract
            )
            nc.sync.dma_start(out=out_rows[:, half * PAIR + tiles.start : half * PAIR + tiles.stop, :], in_=out_sb)

        def biased(half):
            return half == HALVES - 1

        def exists(half):
            return 0 <= half < HALVES

        with tc.manual_schedule(engines={mybir.EngineType.PE, mybir.EngineType.Activation, mybir.EngineType.DVE}):
            idle_ps = psum.tile([P, 512], F32, tag="bank")
            for number in range(4):
                nc.tensor.matmul(idle_ps[:], lhsT=idle[:, 0:P], rhs=idle[:], start=True, stop=True)
            bias_rows_f32 = const.tile([P, P], F32)
            bias_col = const.tile([P, GATE_TILES], F32)
            b_n = const.tile([P, PAIR, HIDDEN], F32)
            for s in range(PAIR):
                transpose_x(0, s)
                copy_x(0, s)
            for s in range(PAIR):
                transpose_x(1, s)
            nc.vector.tensor_copy(out=bias_rows_f32[:], in_=bias_rows[:])
            quantise(0)
            for s in range(PAIR):
                copy_x(1, s)
            bias_ps = psum.tile([P, PAIR, HIDDEN], F32, tag="bank")
            nc.tensor.transpose(bias_ps[:, 0, 0:P], bias_rows_f32[:], ident[:])
            nc.vector.tensor_copy(out=bias_col[:], in_=bias_ps[:, 0, 0:GATE_TILES])
            b_n_ps = psum.tile([P, PAIR, HIDDEN], F32, tag="bank")
            for s in range(PAIR):
                for c in range(HIDDEN // P):
                    row = RZ_TILES + c
                    nc.tensor.matmul(
                        b_n_ps[:, s, c * P : (c + 1) * P],
                        lhsT=ident_bf16[:, row : row + 1].to_broadcast([P, P]),
                        rhs=bias_rows[:],
                        start=True,
                        stop=True,
                    )
            for step in range(HALVES + 1):
                if exists(step + X_LEAD + X_LOAD_LEAD):
                    load_x(step + X_LEAD + X_LOAD_LEAD)
                first_use = step + GH_LOAD_LEAD
                if exists(first_use) and first_use % 2 == 0:
                    load_gh_h(first_use, 2)
                if step > 0 and exists(step):
                    quantise(step)
                if exists(step - PRE_LAG) and not biased(step - PRE_LAG):
                    bias_n(step - PRE_LAG)
                if exists(step - CANDIDATE_LAG):
                    candidate_product(step - CANDIDATE_LAG)
                if exists(step - BLEND_LAG):
                    blend_new(step - BLEND_LAG)
                if exists(step - CANDIDATE_LAG):
                    candidate_sum(step - CANDIDATE_LAG)
                if exists(step - BLEND_LAG):
                    blend_sum(step - BLEND_LAG)
                if exists(step - CANDIDATE_LAG):
                    blend_keep(step - CANDIDATE_LAG)
                for s in range(PAIR):
                    if step > 0 and exists(step + X_LEAD):
                        transpose_x(step + X_LEAD, s)
                for s in range(PAIR):
                    if step > 0 and exists(step + X_LEAD):
                        copy_x(step + X_LEAD, s)
                for s in range(PAIR):
                    if exists(step - ADD_LAG):
                        open_rz(step - ADD_LAG, s)
                for s in range(PAIR):
                    if exists(step - ADD_LAG):
                        add_gh(step - ADD_LAG, s)
                if exists(step - ADD_LAG) and biased(step - ADD_LAG):
                    transpose_n(step - ADD_LAG)
                if exists(step - CANDIDATE_LAG):
                    tanh_n(step - CANDIDATE_LAG)
                if step == 0:
                    nc.vector.tensor_copy(out=b_n[:], in_=b_n_ps[:])
                if exists(step - 1) and step < HALVES:
                    project_n(step - 1)
                if exists(step):
                    project_rz(step)
                if step == HALVES - 1:
                    project_n(step)
            last = HALVES - 1
            candidate_product(last, slice(0, 1))
            candidate_product(last, slice(1, 2))
            blend_keep(last)
            blend_new(last - 1)
            for s in range(PAIR):
                candidate_sum(last, slice(s, s + 1))
            blend_sum(last - 1)
            for s in range(PAIR):
                tanh_n(last, slice(s, s + 1))
            for s in range(PAIR):
                blend_new(last, slice(s, s + 1))
            for s in range(PAIR):
                blend_sum(last, slice(s, s + 1))
